import numpy as np
import ml_dtypes


def mxq(x, axis, fmt="e4m3"):
    dtype, down = {"e4m3": (ml_dtypes.float8_e4m3fn, 7), "e5m2": (ml_dtypes.float8_e5m2, 14)}[fmt]
    v = np.moveaxis(np.asarray(x, np.float32).astype(ml_dtypes.bfloat16).astype(np.float64), axis, -1)
    blocks = v.reshape(v.shape[:-1] + (-1, 32))
    amax = np.abs(blocks).max(-1, keepdims=True)
    byte = np.maximum(np.where(amax > 0, np.frexp(amax)[1] - 1 + 127, 0) - down, 1)
    scale = np.exp2(byte - 127.0)
    codes = (blocks / scale).astype(np.float32).astype(dtype).astype(np.float64)
    return np.moveaxis((codes * scale).reshape(v.shape), -1, axis)


WIDE = False


def mx_kscale(k):
    if not WIDE:
        return np.ones(k)
    levels = np.array([10, -10, 5, -5, 0])
    a = np.random.permutation(np.resize(levels, k // 512 * 4)).reshape(k // 512, 4)
    idx = np.arange(k)
    return np.exp2(a[idx // 512, idx % 128 // 32])


BF16 = ml_dtypes.bfloat16


def bf(x):
    return np.asarray(x, np.float32).astype(BF16)


def f64(x):
    return np.asarray(x).astype(np.float64)


B, D, U = 256, 1024, 1024
KD = 3 * U + D


def setup_inputs():
    s = np.ones(KD)
    s[3 * U:] = np.sort(mx_kscale(KD))[::KD // D]

    def gate():
        return bf(np.random.standard_normal((KD, U)) * 1.25 / np.sqrt(KD) / s[:, None])

    def bias():
        return bf(np.random.standard_normal(U) * 0.5)

    return {"x": bf(np.random.standard_normal((B, D)) * s[3 * U:]),
            "left_state": bf(np.random.standard_normal((B, U))),
            "top_state": bf(np.random.standard_normal((B, U))),
            "diagonal_state": bf(np.random.standard_normal((B, U))),
            "h_cand": bf(np.tanh(np.random.standard_normal((B, U)))),
            "w_zi": gate(), "b_zi": bias(), "w_zl": gate(), "b_zl": bias(),
            "w_zt": gate(), "b_zt": bias(), "w_zd": gate(), "b_zd": bias()}


def reference(x, left_state, top_state, diagonal_state, h_cand, w_zi, b_zi, w_zl, b_zl, w_zt, b_zt, w_zd, b_zd):
    left, top, diag = f64(left_state), f64(top_state), f64(diagonal_state)
    q = np.concatenate([left, top, diag, f64(x)], axis=1)
    W = np.concatenate([f64(w_zi), f64(w_zl), f64(w_zt), f64(w_zd)], axis=1)
    b = np.concatenate([f64(b_zi), f64(b_zl), f64(b_zt), f64(b_zd)])
    g = ((mxq(q, 1, "e4m3") @ mxq(W, 0, "e4m3")) + b).reshape(-1, 4, U)
    e = np.exp(g - g.max(axis=1, keepdims=True))
    z = e / e.sum(axis=1, keepdims=True)
    return z[:, 1] * left + z[:, 2] * top + z[:, 3] * diag + z[:, 0] * f64(h_cand)

@@ -1,0 +1,298 @@
+from contextlib import ExitStack
+
+import concourse.mybir as mybir
+from concourse.masks import make_identity
+
+F32 = mybir.dt.float32
+BF16 = mybir.dt.bfloat16
+I32 = mybir.dt.int32
+U32 = mybir.dt.uint32
+U8 = mybir.dt.uint8
+FP8X4 = mybir.dt.float8_e4m3fn_x4
+ACT = mybir.ActivationFunctionType
+ALU = mybir.AluOpType
+
+P = 128
+PACK = 4
+K_PASS = P * PACK
+BATCH = 256
+UNITS = 1024
+K_ALL = 4 * UNITS
+GATES = 4
+BATCH_TILES = BATCH // P
+PASSES = K_ALL // K_PASS
+ROUND_UNITS = 512
+ROUNDS = UNITS // ROUND_UNITS
+CHUNKS_PER_ROUND = PASSES * GATES
+CHUNKS = ROUNDS * CHUNKS_PER_ROUND
+
+FLOPS = 2 * BATCH * K_ALL * GATES * UNITS
+
+VECTOR_COLS_FIRST_ROUND = 256
+VECTOR_COLS_LATER_ROUNDS = 176
+PREFETCH = 6
+STEP_EVERY = 4
+
+
+def tile_multidimensinalgrucell_pb_kernel(
+    tc, x, left_state, top_state, diagonal_state, h_cand,
+    w_zi, b_zi, w_zl, b_zl, w_zt, b_zt, w_zd, b_zd, out,
+):
+    nc = tc.nc
+    weights = [w_zi, w_zl, w_zt, w_zd]
+    biases = [b_zi, b_zl, b_zt, b_zd]
+    row_sets = [h_cand, left_state, top_state, diagonal_state, x]
+
+    with ExitStack() as stack:
+        stack.enter_context(tc.manual_schedule())
+        keep = stack.enter_context(tc.tile_pool(name="keep", bufs=1))
+        q_stage = stack.enter_context(tc.tile_pool(name="q_stage", bufs=2))
+        raw_pool = stack.enter_context(tc.tile_pool(name="raw", bufs=PREFETCH + 2))
+        grouped_pool = stack.enter_context(tc.tile_pool(name="grouped", bufs=4))
+        code_pool = stack.enter_context(tc.tile_pool(name="codes", bufs=6))
+        per_tile = stack.enter_context(tc.tile_pool(name="per_tile", bufs=2))
+        scratch = stack.enter_context(tc.tile_pool(name="scratch", bufs=1))
+        psum = stack.enter_context(tc.psum_pool(name="psum", bufs=1))
+
+        def bank(shape, dtype, index):
+            return psum.tile(shape, dtype, tag="bank%d" % index, name="bank%d" % index)
+
+        ident_f32 = keep.tile([P, P], F32)
+        make_identity(nc, ident_f32[:])
+        ident_bf16 = keep.tile([P, P], BF16)
+        make_identity(nc, ident_bf16[:])
+
+        bias_rows = keep.tile([P, UNITS], BF16)
+        nc.vector.memset(bias_rows[:].bitcast(I32), 0)
+        for gate in range(GATES):
+            nc.sync.dma_start(out=bias_rows[gate : gate + 1, :], in_=biases[gate].unsqueeze(0))
+
+        rows_in = keep.tile([P, BATCH_TILES, len(row_sets), UNITS], BF16)
+
+        def load_row_set(s):
+            nc.sync.dma_start(
+                out=rows_in[:, :, s, :], in_=row_sets[s].rearrange("(m p) c -> p m c", p=P)
+            )
+
+        for s in range(1, len(row_sets)):
+            load_row_set(s)
+
+        raw_of = {}
+
+        def load_chunk(c):
+            gate = c % GATES
+            g = (c // GATES) % PASSES
+            r = c // CHUNKS_PER_ROUND
+            raw = raw_pool.tile([P, PACK, ROUND_UNITS], BF16)
+            nc.sync.dma_start(
+                out=raw[:],
+                in_=weights[gate][
+                    g * K_PASS : (g + 1) * K_PASS, r * ROUND_UNITS : (r + 1) * ROUND_UNITS
+                ].rearrange("(p t) w -> p t w", t=PACK),
+            )
+            raw_of[c] = raw
+
+        for c in range(PREFETCH):
+            load_chunk(c)
+        load_row_set(0)
+
+        bias_all = keep.tile([P, GATES, UNITS], BF16)
+        for gate in range(GATES):
+            spread = bank([P, UNITS], BF16, gate)
+            for h in range(UNITS // ROUND_UNITS):
+                cols = slice(h * ROUND_UNITS, (h + 1) * ROUND_UNITS)
+                nc.tensor.matmul(
+                    out=spread[:, cols],
+                    lhsT=ident_bf16[:, gate : gate + 1].to_broadcast([P, P]),
+                    rhs=bias_rows[:, cols],
+                    start=True,
+                    stop=True,
+                )
+            nc.scalar.copy(out=bias_all[:, gate, :], in_=spread[:])
+
+        q_codes = keep.tile([P, PASSES, BATCH], U32, align_bytes=64)
+        q_scales = keep.tile([P, PASSES, BATCH], U8, align_bytes=64)
+        words_in = rows_in[:].bitcast(F32)
+        words_per_pass = K_PASS // 2
+        q_grouped_of = {}
+
+        def quantise_q(g):
+            nc.vector.quantize_mx(
+                out=q_codes[:, g, :].bitcast(FP8X4), scales=q_scales[:, g, :], in_=q_grouped_of[g][:]
+            )
+
+        for g in range(PASSES):
+            s = 1 + (g * K_PASS) // UNITS
+            first_word = ((g * K_PASS) % UNITS) // 2
+            turned = bank([P, BATCH_TILES, 2, P], F32, (g + GATES) % 8)
+            for m in range(BATCH_TILES):
+                pass_words = words_in[:, m, s, first_word : first_word + words_per_pass].rearrange(
+                    "b (p u) -> b u p", u=2
+                )
+                for u in range(2):
+                    nc.tensor.transpose(turned[:, m, u, :], pass_words[:, u, :], ident_f32[:])
+            q_grouped = q_stage.tile([P, BATCH * PACK], BF16, align_bytes=64)
+            side_by_side = q_grouped[:].bitcast(F32).rearrange("p (m b u) -> p m b u", m=BATCH_TILES, u=2)
+            if g % 2 == 0:
+                nc.vector.tensor_copy(out=side_by_side, in_=turned[:].rearrange("p m u b -> p m b u"))
+            else:
+                nc.scalar.copy(out=side_by_side, in_=turned[:].rearrange("p m u b -> p m b u"))
+            q_grouped_of[g] = q_grouped
+            if g >= 1:
+                quantise_q(g - 1)
+        quantise_q(PASSES - 1)
+
+        grouped_of = {}
+        codes_of = {}
+        sums = {}
+
+        def regroup(c):
+            r = c // CHUNKS_PER_ROUND
+            split = VECTOR_COLS_FIRST_ROUND if r == 0 else VECTOR_COLS_LATER_ROUNDS
+            raw = raw_of[c]
+            grouped = grouped_pool.tile([P, ROUND_UNITS, PACK], BF16, align_bytes=64)
+            nc.vector.tensor_copy(
+                out=grouped[:, 0:split, :].rearrange("p (c i) t -> p c t i", i=4),
+                in_=raw[:, :, 0:split].rearrange("p t (c i) -> p c t i", i=4),
+            )
+            nc.scalar.copy(
+                out=grouped[:, split:ROUND_UNITS, :].rearrange("p (c i) t -> p c t i", i=4),
+                in_=raw[:, :, split:ROUND_UNITS].rearrange("p t (c i) -> p c t i", i=4),
+            )
+            grouped_of[c] = grouped
+
+        def quantise(c):
+            w_codes = code_pool.tile([P, ROUND_UNITS], U32, align_bytes=64)
+            w_scales = code_pool.tile([P, ROUND_UNITS], U8, align_bytes=64)
+            nc.vector.quantize_mx(
+                out=w_codes[:].bitcast(FP8X4),
+                scales=w_scales[:],
+                in_=grouped_of[c][:].rearrange("p w t -> p (w t)"),
+            )
+            codes_of[c] = (w_codes, w_scales)
+
+        def multiply(c):
+            gate = c % GATES
+            g = (c // GATES) % PASSES
+            w_codes, w_scales = codes_of[c]
+            for m in range(BATCH_TILES):
+                if g == 0:
+                    sums[(m, gate)] = bank([P, ROUND_UNITS], F32, m * GATES + gate)
+                rows = slice(m * P, (m + 1) * P)
+                nc.tensor.matmul_mx(
+                    out=sums[(m, gate)][:],
+                    lhsT=q_codes[:, g, rows].bitcast(FP8X4),
+                    lhsT_scale=q_scales[:, g, rows],
+                    rhs=w_codes[:].bitcast(FP8X4),
+                    rhs_scale=w_scales[:],
+                    start=(g == 0),
+                    stop=(g == PASSES - 1),
+                )
+
+        def softmax_and_blend(r):
+            cols = slice(r * ROUND_UNITS, (r + 1) * ROUND_UNITS)
+            logits = {}
+            weight = {}
+            below = scratch.tile([P, BATCH_TILES, ROUND_UNITS], F32, name="below")
+            above = scratch.tile([P, BATCH_TILES, ROUND_UNITS], F32, name="above")
+            log_below = scratch.tile([P, BATCH_TILES, ROUND_UNITS], F32, name="log_below")
+            one_over = scratch.tile([P, BATCH_TILES, ROUND_UNITS], F32, name="one_over")
+            result = scratch.tile([P, BATCH_TILES, ROUND_UNITS], F32, name="result")
+
+            for m in range(BATCH_TILES):
+                logits[m] = per_tile.tile([P, GATES, ROUND_UNITS], F32, name="logits")
+                for gate in range(GATES):
+                    nc.vector.tensor_tensor(
+                        out=logits[m][:, gate, :],
+                        in0=sums[(m, gate)][:],
+                        in1=bias_all[:, gate, cols],
+                        op=ALU.add,
+                    )
+
+            def subtract_max(m):
+                pair_max = scratch.tile([P, 2, ROUND_UNITS], F32, name="pair_max")
+                top = scratch.tile([P, ROUND_UNITS], F32, name="top")
+                nc.vector.tensor_tensor(
+                    out=pair_max[:], in0=logits[m][:, 0:2, :], in1=logits[m][:, 2:4, :], op=ALU.max
+                )
+                nc.vector.tensor_tensor(
+                    out=top[:], in0=pair_max[:, 0, :], in1=pair_max[:, 1, :], op=ALU.max
+                )
+                nc.vector.tensor_tensor(
+                    out=logits[m][:],
+                    in0=logits[m][:],
+                    in1=top[:].unsqueeze(1).to_broadcast([P, GATES, ROUND_UNITS]),
+                    op=ALU.subtract,
+                )
+
+            def exponentials(m):
+                weight[m] = per_tile.tile([P, GATES, ROUND_UNITS], F32, name="weight")
+                nc.scalar.activation(out=weight[m][:], in_=logits[m][:], func=ACT.Exp)
+
+            def add_gates(total, terms):
+                pair_sum = scratch.tile([P, 2, ROUND_UNITS], F32, name="pair_sum")
+                nc.vector.tensor_tensor(
+                    out=pair_sum[:], in0=terms[:, 0:2, :], in1=terms[:, 2:4, :], op=ALU.add
+                )
+                nc.vector.tensor_tensor(
+                    out=total, in0=pair_sum[:, 0, :], in1=pair_sum[:, 1, :], op=ALU.add
+                )
+
+            def denominator(m):
+                add_gates(below[:, m, :], weight[m])
+
+            def numerator(m):
+                weighted = scratch.tile([P, GATES, ROUND_UNITS], F32, name="weighted")
+                nc.vector.tensor_tensor(
+                    out=weighted[:], in0=weight[m][:], in1=rows_in[:, m, 0:GATES, cols], op=ALU.mult
+                )
+                add_gates(above[:, m, :], weighted)
+
+            def reciprocal():
+                nc.scalar.activation(out=log_below[:], in_=below[:], func=ACT.Ln)
+                nc.scalar.activation(out=one_over[:], in_=log_below[:], func=ACT.Exp, scale=-1.0)
+
+            def divide_and_store():
+                nc.vector.tensor_tensor(out=result[:], in0=above[:], in1=one_over[:], op=ALU.mult)
+                nc.sync.dma_start(
+                    out=out[:, cols].rearrange("(m p) c -> p m c", p=P), in_=result[:]
+                )
+
+            def step_1():
+                subtract_max(0)
+
+            def step_2():
+                exponentials(0)
+                subtract_max(1)
+
+            def step_3():
+                exponentials(1)
+                denominator(0)
+                numerator(0)
+
+            def step_4():
+                denominator(1)
+
+            def step_5():
+                reciprocal()
+                numerator(1)
+
+            return [step_1, step_2, step_3, step_4, step_5, divide_and_store]
+
+        steps = []
+        for c in range(CHUNKS + 2):
+            if c + PREFETCH < CHUNKS:
+                load_chunk(c + PREFETCH)
+            if c < CHUNKS:
+                regroup(c)
+            if 1 <= c <= CHUNKS:
+                quantise(c - 1)
+            if c >= 2:
+                multiply(c - 2)
+                if (c - 2) % CHUNKS_PER_ROUND == CHUNKS_PER_ROUND - 1:
+                    steps = softmax_and_blend((c - 2) // CHUNKS_PER_ROUND)
+            if steps and c % STEP_EVERY == 0:
+                steps[0]()
+                steps = steps[1:]
+        for step in steps:
+            step()

@@ -30,7 +30,7 @@ FLOPS = 2 * BATCH * K_ALL * GATES * UNITS
 
 VECTOR_COLS_FIRST_ROUND = 256
 VECTOR_COLS_LATER_ROUNDS = 176
-PREFETCH = 6
+PREFETCH = 8
 STEP_EVERY = 4
 
 
@@ -48,7 +48,7 @@ def tile_multidimensinalgrucell_pb_kernel(
         keep = stack.enter_context(tc.tile_pool(name="keep", bufs=1))
         q_stage = stack.enter_context(tc.tile_pool(name="q_stage", bufs=2))
         raw_pool = stack.enter_context(tc.tile_pool(name="raw", bufs=PREFETCH + 2))
-        grouped_pool = stack.enter_context(tc.tile_pool(name="grouped", bufs=4))
+        grouped_pool = stack.enter_context(tc.tile_pool(name="grouped", bufs=6))
         code_pool = stack.enter_context(tc.tile_pool(name="codes", bufs=6))
         per_tile = stack.enter_context(tc.tile_pool(name="per_tile", bufs=2))
         scratch = stack.enter_context(tc.tile_pool(name="scratch", bufs=1))
@@ -67,11 +67,11 @@ def tile_multidimensinalgrucell_pb_kernel(
         for gate in range(GATES):
             nc.sync.dma_start(out=bias_rows[gate : gate + 1, :], in_=biases[gate].unsqueeze(0))
 
-        rows_in = keep.tile([P, BATCH_TILES, len(row_sets), UNITS], BF16)
+        rows_in = keep.tile([P, len(row_sets), BATCH_TILES, UNITS], BF16)
 
         def load_row_set(s):
             nc.sync.dma_start(
-                out=rows_in[:, :, s, :], in_=row_sets[s].rearrange("(m p) c -> p m c", p=P)
+                out=rows_in[:, s, :, :], in_=row_sets[s].rearrange("(m p) c -> p m c", p=P)
             )
 
         for s in range(1, len(row_sets)):
@@ -126,7 +126,7 @@ def tile_multidimensinalgrucell_pb_kernel(
             first_word = ((g * K_PASS) % UNITS) // 2
             turned = bank([P, BATCH_TILES, 2, P], F32, (g + GATES) % 8)
             for m in range(BATCH_TILES):
-                pass_words = words_in[:, m, s, first_word : first_word + words_per_pass].rearrange(
+                pass_words = words_in[:, s, m, first_word : first_word + words_per_pass].rearrange(
                     "b (p u) -> b u p", u=2
                 )
                 for u in range(2):
@@ -244,7 +244,7 @@ def tile_multidimensinalgrucell_pb_kernel(
             def numerator(m):
                 weighted = scratch.tile([P, GATES, ROUND_UNITS], F32, name="weighted")
                 nc.vector.tensor_tensor(
-                    out=weighted[:], in0=weight[m][:], in1=rows_in[:, m, 0:GATES, cols], op=ALU.mult
+                    out=weighted[:], in0=weight[m][:], in1=rows_in[:, 0:GATES, m, cols], op=ALU.mult
                 )
                 add_gates(above[:, m, :], weighted)
 

@@ -94,21 +94,27 @@ def tile_multidimensinalgrucell_pb_kernel(
 
         for c in range(PREFETCH):
             load_chunk(c)
-        load_row_set(0)
 
-        bias_all = keep.tile([P, GATES, UNITS], BF16)
-        for gate in range(GATES):
-            spread = bank([P, UNITS], BF16, gate)
-            for h in range(UNITS // ROUND_UNITS):
-                cols = slice(h * ROUND_UNITS, (h + 1) * ROUND_UNITS)
+        pick = keep.tile([P, GATES], BF16)
+        nc.vector.tensor_tensor(
+            out=pick[:],
+            in0=ident_bf16[:, 0:GATES],
+            in1=ident_bf16[:, 0:1].to_broadcast([P, GATES]),
+            op=ALU.subtract,
+        )
+        bias_gap = keep.tile([P, GATES, UNITS], F32)
+        for gate in range(1, GATES):
+            for r in range(ROUNDS):
+                cols = slice(r * ROUND_UNITS, (r + 1) * ROUND_UNITS)
+                spread = bank([P, ROUND_UNITS], F32, (gate - 1) * ROUNDS + r)
                 nc.tensor.matmul(
-                    out=spread[:, cols],
-                    lhsT=ident_bf16[:, gate : gate + 1].to_broadcast([P, P]),
+                    out=spread[:],
+                    lhsT=pick[:, gate : gate + 1].to_broadcast([P, P]),
                     rhs=bias_rows[:, cols],
                     start=True,
                     stop=True,
                 )
-            nc.scalar.copy(out=bias_all[:, gate, :], in_=spread[:])
+                nc.scalar.copy(out=bias_gap[:, gate, cols], in_=spread[:])
 
         q_codes = keep.tile([P, PASSES, BATCH], U32, align_bytes=64)
         q_scales = keep.tile([P, PASSES, BATCH], U8, align_bytes=64)
@@ -124,7 +130,7 @@ def tile_multidimensinalgrucell_pb_kernel(
         for g in range(PASSES):
             s = 1 + (g * K_PASS) // UNITS
             first_word = ((g * K_PASS) % UNITS) // 2
-            turned = bank([P, BATCH_TILES, 2, P], F32, (g + GATES) % 8)
+            turned = bank([P, BATCH_TILES, 2, P], F32, (g + 6) % 8)
             for m in range(BATCH_TILES):
                 pass_words = words_in[:, s, m, first_word : first_word + words_per_pass].rearrange(
                     "b (p u) -> b u p", u=2
@@ -201,11 +207,12 @@ def tile_multidimensinalgrucell_pb_kernel(
 
             for m in range(BATCH_TILES):
                 logits[m] = per_tile.tile([P, GATES, ROUND_UNITS], F32, name="logits")
-                for gate in range(GATES):
+                nc.scalar.copy(out=logits[m][:, 0, :], in_=sums[(m, 0)][:])
+                for gate in range(1, GATES):
                     nc.vector.tensor_tensor(
                         out=logits[m][:, gate, :],
                         in0=sums[(m, gate)][:],
-                        in1=bias_all[:, gate, cols],
+                        in1=bias_gap[:, gate, cols],
                         op=ALU.add,
                     )
 
@@ -253,10 +260,11 @@ def tile_multidimensinalgrucell_pb_kernel(
                 nc.scalar.activation(out=one_over[:], in_=log_below[:], func=ACT.Exp, scale=-1.0)
 
             def divide_and_store():
-                nc.vector.tensor_tensor(out=result[:], in0=above[:], in1=one_over[:], op=ALU.mult)
-                nc.sync.dma_start(
-                    out=out[:, cols].rearrange("(m p) c -> p m c", p=P), in_=result[:]
-                )
+                for m in range(BATCH_TILES):
+                    nc.vector.tensor_tensor(
+                        out=result[:, m, :], in0=above[:, m, :], in1=one_over[:, m, :], op=ALU.mult
+                    )
+                    nc.sync.dma_start(out=out[m * P : (m + 1) * P, cols], in_=result[:, m, :])
 
             def step_1():
                 subtract_max(0)
@@ -283,6 +291,8 @@ def tile_multidimensinalgrucell_pb_kernel(
         for c in range(CHUNKS + 2):
             if c + PREFETCH < CHUNKS:
                 load_chunk(c + PREFETCH)
+            if c + PREFETCH == CHUNKS_PER_ROUND:
+                load_row_set(0)
             if c < CHUNKS:
                 regroup(c)
             if 1 <= c <= CHUNKS:

@@ -21,17 +21,17 @@ K_ALL = 4 * UNITS
 GATES = 4
 BATCH_TILES = BATCH // P
 PASSES = K_ALL // K_PASS
+BANKS = 8
 ROUND_UNITS = 512
 ROUNDS = UNITS // ROUND_UNITS
-CHUNKS_PER_ROUND = PASSES * GATES
-CHUNKS = ROUNDS * CHUNKS_PER_ROUND
 
 FLOPS = 2 * BATCH * K_ALL * GATES * UNITS
 
-VECTOR_COLS_FIRST_ROUND = 256
-VECTOR_COLS_LATER_ROUNDS = 176
+WIDE_PASSES = 5
+VECTOR_COLS = 256
+VECTOR_COLS_BESIDE_SOFTMAX = 64
 PREFETCH = 8
-STEP_EVERY = 4
+STEP_EVERY = 2
 
 
 def tile_multidimensinalgrucell_pb_kernel(
@@ -43,12 +43,23 @@ def tile_multidimensinalgrucell_pb_kernel(
     biases = [b_zi, b_zl, b_zt, b_zd]
     row_sets = [h_cand, left_state, top_state, diagonal_state, x]
 
+    pieces = []
+    for g in range(PASSES):
+        for gate in range(GATES):
+            pieces.append((g, gate, 0))
+            if g < WIDE_PASSES:
+                pieces.append((g, gate, 1))
+    first_round_pieces = len(pieces)
+    for g in range(WIDE_PASSES, PASSES):
+        for gate in range(GATES):
+            pieces.append((g, gate, 1))
+
     with ExitStack() as stack:
         stack.enter_context(tc.manual_schedule())
         keep = stack.enter_context(tc.tile_pool(name="keep", bufs=1))
         q_stage = stack.enter_context(tc.tile_pool(name="q_stage", bufs=2))
-        raw_pool = stack.enter_context(tc.tile_pool(name="raw", bufs=PREFETCH + 2))
-        grouped_pool = stack.enter_context(tc.tile_pool(name="grouped", bufs=6))
+        raw_pool = stack.enter_context(tc.tile_pool(name="raw", bufs=5))
+        grouped_pool = stack.enter_context(tc.tile_pool(name="grouped", bufs=4))
         code_pool = stack.enter_context(tc.tile_pool(name="codes", bufs=6))
         per_tile = stack.enter_context(tc.tile_pool(name="per_tile", bufs=2))
         scratch = stack.enter_context(tc.tile_pool(name="scratch", bufs=1))
@@ -79,21 +90,28 @@ def tile_multidimensinalgrucell_pb_kernel(
 
         raw_of = {}
 
-        def load_chunk(c):
-            gate = c % GATES
-            g = (c // GATES) % PASSES
-            r = c // CHUNKS_PER_ROUND
-            raw = raw_pool.tile([P, PACK, ROUND_UNITS], BF16)
-            nc.sync.dma_start(
-                out=raw[:],
-                in_=weights[gate][
-                    g * K_PASS : (g + 1) * K_PASS, r * ROUND_UNITS : (r + 1) * ROUND_UNITS
-                ].rearrange("(p t) w -> p t w", t=PACK),
-            )
-            raw_of[c] = raw
+        def load_for(piece):
+            g, gate, r = piece
+            k_rows = weights[gate][g * K_PASS : (g + 1) * K_PASS, :]
+            if g >= WIDE_PASSES:
+                raw = raw_pool.tile([P, PACK, ROUND_UNITS], BF16, tag="raw")
+                nc.sync.dma_start(
+                    out=raw[:],
+                    in_=k_rows[:, r * ROUND_UNITS : (r + 1) * ROUND_UNITS].rearrange(
+                        "(p t) w -> p t w", t=PACK
+                    ),
+                )
+                raw_of[piece] = raw[:]
+            elif r == 0:
+                raw = raw_pool.tile([P, PACK, UNITS], BF16, tag="raw")
+                nc.sync.dma_start(out=raw[:], in_=k_rows.rearrange("(p t) w -> p t w", t=PACK))
+                for each_round in range(ROUNDS):
+                    raw_of[(g, gate, each_round)] = raw[
+                        :, :, each_round * ROUND_UNITS : (each_round + 1) * ROUND_UNITS
+                    ]
 
         for c in range(PREFETCH):
-            load_chunk(c)
+            load_for(pieces[c])
 
         pick = keep.tile([P, GATES], BF16)
         nc.vector.tensor_tensor(
@@ -102,11 +120,13 @@ def tile_multidimensinalgrucell_pb_kernel(
             in1=ident_bf16[:, 0:1].to_broadcast([P, GATES]),
             op=ALU.subtract,
         )
-        bias_gap = keep.tile([P, GATES, UNITS], F32)
+        bias_gap = keep.tile([P, GATES - 1, UNITS], F32)
+        banks_used = 0
         for gate in range(1, GATES):
             for r in range(ROUNDS):
                 cols = slice(r * ROUND_UNITS, (r + 1) * ROUND_UNITS)
-                spread = bank([P, ROUND_UNITS], F32, (gate - 1) * ROUNDS + r)
+                spread = bank([P, ROUND_UNITS], F32, banks_used % BANKS)
+                banks_used += 1
                 nc.tensor.matmul(
                     out=spread[:],
                     lhsT=pick[:, gate : gate + 1].to_broadcast([P, P]),
@@ -114,7 +134,7 @@ def tile_multidimensinalgrucell_pb_kernel(
                     start=True,
                     stop=True,
                 )
-                nc.scalar.copy(out=bias_gap[:, gate, cols], in_=spread[:])
+                nc.scalar.copy(out=bias_gap[:, gate - 1, cols], in_=spread[:])
 
         q_codes = keep.tile([P, PASSES, BATCH], U32, align_bytes=64)
         q_scales = keep.tile([P, PASSES, BATCH], U8, align_bytes=64)
@@ -130,7 +150,8 @@ def tile_multidimensinalgrucell_pb_kernel(
         for g in range(PASSES):
             s = 1 + (g * K_PASS) // UNITS
             first_word = ((g * K_PASS) % UNITS) // 2
-            turned = bank([P, BATCH_TILES, 2, P], F32, (g + 6) % 8)
+            turned = bank([P, BATCH_TILES, 2, P], F32, banks_used % BANKS)
+            banks_used += 1
             for m in range(BATCH_TILES):
                 pass_words = words_in[:, s, m, first_word : first_word + words_per_pass].rearrange(
                     "b (p u) -> b u p", u=2
@@ -148,39 +169,49 @@ def tile_multidimensinalgrucell_pb_kernel(
                 quantise_q(g - 1)
         quantise_q(PASSES - 1)
 
+        kept_codes = keep.tile([P, WIDE_PASSES * GATES, ROUND_UNITS], U32, align_bytes=64)
+        kept_scales = keep.tile([P, WIDE_PASSES * GATES, ROUND_UNITS], U8, align_bytes=64)
         grouped_of = {}
         codes_of = {}
         sums = {}
 
-        def regroup(c):
-            r = c // CHUNKS_PER_ROUND
-            split = VECTOR_COLS_FIRST_ROUND if r == 0 else VECTOR_COLS_LATER_ROUNDS
-            raw = raw_of[c]
+        def is_kept(piece):
+            g, gate, r = piece
+            return r == 1 and g < WIDE_PASSES
+
+        def regroup(piece, vector_cols):
+            raw = raw_of[piece]
             grouped = grouped_pool.tile([P, ROUND_UNITS, PACK], BF16, align_bytes=64)
             nc.vector.tensor_copy(
-                out=grouped[:, 0:split, :].rearrange("p (c i) t -> p c t i", i=4),
-                in_=raw[:, :, 0:split].rearrange("p t (c i) -> p c t i", i=4),
+                out=grouped[:, 0:vector_cols, :].rearrange("p (c i) t -> p c t i", i=4),
+                in_=raw[:, :, 0:vector_cols].rearrange("p t (c i) -> p c t i", i=4),
             )
             nc.scalar.copy(
-                out=grouped[:, split:ROUND_UNITS, :].rearrange("p (c i) t -> p c t i", i=4),
-                in_=raw[:, :, split:ROUND_UNITS].rearrange("p t (c i) -> p c t i", i=4),
+                out=grouped[:, vector_cols:ROUND_UNITS, :].rearrange("p (c i) t -> p c t i", i=4),
+                in_=raw[:, :, vector_cols:ROUND_UNITS].rearrange("p t (c i) -> p c t i", i=4),
             )
-            grouped_of[c] = grouped
+            grouped_of[piece] = grouped
 
-        def quantise(c):
-            w_codes = code_pool.tile([P, ROUND_UNITS], U32, align_bytes=64)
-            w_scales = code_pool.tile([P, ROUND_UNITS], U8, align_bytes=64)
+        def quantise(piece):
+            g, gate, r = piece
+            if is_kept(piece):
+                w_codes = kept_codes[:, g * GATES + gate, :]
+                w_scales = kept_scales[:, g * GATES + gate, :]
+            else:
+                codes_tile = code_pool.tile([P, ROUND_UNITS], U32, align_bytes=64)
+                scales_tile = code_pool.tile([P, ROUND_UNITS], U8, align_bytes=64)
+                w_codes = codes_tile[:]
+                w_scales = scales_tile[:]
             nc.vector.quantize_mx(
-                out=w_codes[:].bitcast(FP8X4),
-                scales=w_scales[:],
-                in_=grouped_of[c][:].rearrange("p w t -> p (w t)"),
+                out=w_codes.bitcast(FP8X4),
+                scales=w_scales,
+                in_=grouped_of[piece][:].rearrange("p w t -> p (w t)"),
             )
-            codes_of[c] = (w_codes, w_scales)
+            codes_of[piece] = (w_codes, w_scales)
 
-        def multiply(c):
-            gate = c % GATES
-            g = (c // GATES) % PASSES
-            w_codes, w_scales = codes_of[c]
+        def multiply(piece):
+            g, gate, r = piece
+            w_codes, w_scales = codes_of[piece]
             for m in range(BATCH_TILES):
                 if g == 0:
                     sums[(m, gate)] = bank([P, ROUND_UNITS], F32, m * GATES + gate)
@@ -189,8 +220,8 @@ def tile_multidimensinalgrucell_pb_kernel(
                     out=sums[(m, gate)][:],
                     lhsT=q_codes[:, g, rows].bitcast(FP8X4),
                     lhsT_scale=q_scales[:, g, rows],
-                    rhs=w_codes[:].bitcast(FP8X4),
-                    rhs_scale=w_scales[:],
+                    rhs=w_codes.bitcast(FP8X4),
+                    rhs_scale=w_scales,
                     start=(g == 0),
                     stop=(g == PASSES - 1),
                 )
@@ -201,9 +232,6 @@ def tile_multidimensinalgrucell_pb_kernel(
             weight = {}
             below = scratch.tile([P, BATCH_TILES, ROUND_UNITS], F32, name="below")
             above = scratch.tile([P, BATCH_TILES, ROUND_UNITS], F32, name="above")
-            log_below = scratch.tile([P, BATCH_TILES, ROUND_UNITS], F32, name="log_below")
-            one_over = scratch.tile([P, BATCH_TILES, ROUND_UNITS], F32, name="one_over")
-            result = scratch.tile([P, BATCH_TILES, ROUND_UNITS], F32, name="result")
 
             for m in range(BATCH_TILES):
                 logits[m] = per_tile.tile([P, GATES, ROUND_UNITS], F32, name="logits")
@@ -212,12 +240,12 @@ def tile_multidimensinalgrucell_pb_kernel(
                     nc.vector.tensor_tensor(
                         out=logits[m][:, gate, :],
                         in0=sums[(m, gate)][:],
-                        in1=bias_gap[:, gate, cols],
+                        in1=bias_gap[:, gate - 1, cols],
                         op=ALU.add,
                     )
 
             def subtract_max(m):
-                pair_max = scratch.tile([P, 2, ROUND_UNITS], F32, name="pair_max")
+                pair_max = scratch.tile([P, 2, ROUND_UNITS], F32, name="pair")
                 top = scratch.tile([P, ROUND_UNITS], F32, name="top")
                 nc.vector.tensor_tensor(
                     out=pair_max[:], in0=logits[m][:, 0:2, :], in1=logits[m][:, 2:4, :], op=ALU.max
@@ -237,7 +265,7 @@ def tile_multidimensinalgrucell_pb_kernel(
                 nc.scalar.activation(out=weight[m][:], in_=logits[m][:], func=ACT.Exp)
 
             def add_gates(total, terms):
-                pair_sum = scratch.tile([P, 2, ROUND_UNITS], F32, name="pair_sum")
+                pair_sum = scratch.tile([P, 2, ROUND_UNITS], F32, name="pair")
                 nc.vector.tensor_tensor(
                     out=pair_sum[:], in0=terms[:, 0:2, :], in1=terms[:, 2:4, :], op=ALU.add
                 )
@@ -249,22 +277,21 @@ def tile_multidimensinalgrucell_pb_kernel(
                 add_gates(below[:, m, :], weight[m])
 
             def numerator(m):
-                weighted = scratch.tile([P, GATES, ROUND_UNITS], F32, name="weighted")
                 nc.vector.tensor_tensor(
-                    out=weighted[:], in0=weight[m][:], in1=rows_in[:, 0:GATES, m, cols], op=ALU.mult
+                    out=weight[m][:], in0=weight[m][:], in1=rows_in[:, 0:GATES, m, cols], op=ALU.mult
                 )
-                add_gates(above[:, m, :], weighted)
+                add_gates(above[:, m, :], weight[m])
 
             def reciprocal():
-                nc.scalar.activation(out=log_below[:], in_=below[:], func=ACT.Ln)
-                nc.scalar.activation(out=one_over[:], in_=log_below[:], func=ACT.Exp, scale=-1.0)
+                nc.scalar.activation(out=below[:], in_=below[:], func=ACT.Ln)
+                nc.scalar.activation(out=below[:], in_=below[:], func=ACT.Exp, scale=-1.0)
 
             def divide_and_store():
                 for m in range(BATCH_TILES):
                     nc.vector.tensor_tensor(
-                        out=result[:, m, :], in0=above[:, m, :], in1=one_over[:, m, :], op=ALU.mult
+                        out=above[:, m, :], in0=above[:, m, :], in1=below[:, m, :], op=ALU.mult
                     )
-                    nc.sync.dma_start(out=out[m * P : (m + 1) * P, cols], in_=result[:, m, :])
+                    nc.sync.dma_start(out=out[m * P : (m + 1) * P, cols], in_=above[:, m, :])
 
             def step_1():
                 subtract_max(0)
@@ -288,19 +315,24 @@ def tile_multidimensinalgrucell_pb_kernel(
             return [step_1, step_2, step_3, step_4, step_5, divide_and_store]
 
         steps = []
-        for c in range(CHUNKS + 2):
-            if c + PREFETCH < CHUNKS:
-                load_chunk(c + PREFETCH)
-            if c + PREFETCH == CHUNKS_PER_ROUND:
+        for c in range(len(pieces) + 2):
+            if c + PREFETCH < len(pieces):
+                load_for(pieces[c + PREFETCH])
+            if c + PREFETCH == first_round_pieces:
                 load_row_set(0)
-            if c < CHUNKS:
-                regroup(c)
-            if 1 <= c <= CHUNKS:
-                quantise(c - 1)
-            if c >= 2:
-                multiply(c - 2)
-                if (c - 2) % CHUNKS_PER_ROUND == CHUNKS_PER_ROUND - 1:
-                    steps = softmax_and_blend((c - 2) // CHUNKS_PER_ROUND)
+            if c < len(pieces):
+                regroup(pieces[c], VECTOR_COLS_BESIDE_SOFTMAX if steps else VECTOR_COLS)
+            if 1 <= c <= len(pieces):
+                quantise(pieces[c - 1])
+            if c >= 2 and not is_kept(pieces[c - 2]):
+                multiply(pieces[c - 2])
+            if c - 2 == first_round_pieces - 1:
+                steps = softmax_and_blend(0)
+                for piece in pieces[0:first_round_pieces]:
+                    if is_kept(piece):
+                        multiply(piece)
+            if c - 2 == len(pieces) - 1:
+                steps = softmax_and_blend(1)
             if steps and c % STEP_EVERY == 0:
                 steps[0]()
                 steps = steps[1:]

@@ -21,17 +21,17 @@ K_ALL = 4 * UNITS
 GATES = 4
 BATCH_TILES = BATCH // P
 PASSES = K_ALL // K_PASS
-BANKS = 8
 ROUND_UNITS = 512
 ROUNDS = UNITS // ROUND_UNITS
+CHUNKS_PER_ROUND = PASSES * GATES
+CHUNKS = ROUNDS * CHUNKS_PER_ROUND
 
 FLOPS = 2 * BATCH * K_ALL * GATES * UNITS
 
-WIDE_PASSES = 5
-VECTOR_COLS = 256
-VECTOR_COLS_BESIDE_SOFTMAX = 64
+VECTOR_COLS_FIRST_ROUND = 240
+VECTOR_COLS_LATER_ROUNDS = 176
 PREFETCH = 8
-STEP_EVERY = 2
+STEP_EVERY = 4
 
 
 def tile_multidimensinalgrucell_pb_kernel(
@@ -43,24 +43,13 @@ def tile_multidimensinalgrucell_pb_kernel(
     biases = [b_zi, b_zl, b_zt, b_zd]
     row_sets = [h_cand, left_state, top_state, diagonal_state, x]
 
-    pieces = []
-    for g in range(PASSES):
-        for gate in range(GATES):
-            pieces.append((g, gate, 0))
-            if g < WIDE_PASSES:
-                pieces.append((g, gate, 1))
-    first_round_pieces = len(pieces)
-    for g in range(WIDE_PASSES, PASSES):
-        for gate in range(GATES):
-            pieces.append((g, gate, 1))
-
     with ExitStack() as stack:
         stack.enter_context(tc.manual_schedule())
         keep = stack.enter_context(tc.tile_pool(name="keep", bufs=1))
         q_stage = stack.enter_context(tc.tile_pool(name="q_stage", bufs=2))
-        raw_pool = stack.enter_context(tc.tile_pool(name="raw", bufs=5))
-        grouped_pool = stack.enter_context(tc.tile_pool(name="grouped", bufs=4))
-        code_pool = stack.enter_context(tc.tile_pool(name="codes", bufs=6))
+        raw_pool = stack.enter_context(tc.tile_pool(name="raw", bufs=PREFETCH + 2))
+        grouped_pool = stack.enter_context(tc.tile_pool(name="grouped", bufs=6))
+        code_pool = stack.enter_context(tc.tile_pool(name="codes", bufs=PASSES + 4))
         per_tile = stack.enter_context(tc.tile_pool(name="per_tile", bufs=2))
         scratch = stack.enter_context(tc.tile_pool(name="scratch", bufs=1))
         psum = stack.enter_context(tc.psum_pool(name="psum", bufs=1))
@@ -85,33 +74,25 @@ def tile_multidimensinalgrucell_pb_kernel(
                 out=rows_in[:, s, :, :], in_=row_sets[s].rearrange("(m p) c -> p m c", p=P)
             )
 
-        for s in range(1, len(row_sets)):
-            load_row_set(s)
-
         raw_of = {}
 
-        def load_for(piece):
-            g, gate, r = piece
-            k_rows = weights[gate][g * K_PASS : (g + 1) * K_PASS, :]
-            if g >= WIDE_PASSES:
-                raw = raw_pool.tile([P, PACK, ROUND_UNITS], BF16, tag="raw")
-                nc.sync.dma_start(
-                    out=raw[:],
-                    in_=k_rows[:, r * ROUND_UNITS : (r + 1) * ROUND_UNITS].rearrange(
-                        "(p t) w -> p t w", t=PACK
-                    ),
-                )
-                raw_of[piece] = raw[:]
-            elif r == 0:
-                raw = raw_pool.tile([P, PACK, UNITS], BF16, tag="raw")
-                nc.sync.dma_start(out=raw[:], in_=k_rows.rearrange("(p t) w -> p t w", t=PACK))
-                for each_round in range(ROUNDS):
-                    raw_of[(g, gate, each_round)] = raw[
-                        :, :, each_round * ROUND_UNITS : (each_round + 1) * ROUND_UNITS
-                    ]
+        def load_chunk(c):
+            gate = c % GATES
+            g = (c // GATES) % PASSES
+            r = c // CHUNKS_PER_ROUND
+            raw = raw_pool.tile([P, PACK, ROUND_UNITS], BF16)
+            nc.sync.dma_start(
+                out=raw[:],
+                in_=weights[gate][
+                    g * K_PASS : (g + 1) * K_PASS, r * ROUND_UNITS : (r + 1) * ROUND_UNITS
+                ].rearrange("(p t) w -> p t w", t=PACK),
+            )
+            raw_of[c] = raw
 
         for c in range(PREFETCH):
-            load_for(pieces[c])
+            load_chunk(c)
+            if c + 1 < len(row_sets):
+                load_row_set(c + 1)
 
         pick = keep.tile([P, GATES], BF16)
         nc.vector.tensor_tensor(
@@ -121,12 +102,10 @@ def tile_multidimensinalgrucell_pb_kernel(
             op=ALU.subtract,
         )
         bias_gap = keep.tile([P, GATES - 1, UNITS], F32)
-        banks_used = 0
         for gate in range(1, GATES):
             for r in range(ROUNDS):
                 cols = slice(r * ROUND_UNITS, (r + 1) * ROUND_UNITS)
-                spread = bank([P, ROUND_UNITS], F32, banks_used % BANKS)
-                banks_used += 1
+                spread = bank([P, ROUND_UNITS], F32, (gate - 1) * ROUNDS + r)
                 nc.tensor.matmul(
                     out=spread[:],
                     lhsT=pick[:, gate : gate + 1].to_broadcast([P, P]),
@@ -147,11 +126,10 @@ def tile_multidimensinalgrucell_pb_kernel(
                 out=q_codes[:, g, :].bitcast(FP8X4), scales=q_scales[:, g, :], in_=q_grouped_of[g][:]
             )
 
-        for g in range(PASSES):
+        def turn_q(g):
             s = 1 + (g * K_PASS) // UNITS
             first_word = ((g * K_PASS) % UNITS) // 2
-            turned = bank([P, BATCH_TILES, 2, P], F32, banks_used % BANKS)
-            banks_used += 1
+            turned = bank([P, BATCH_TILES, 2, P], F32, (g + 6) % 8)
             for m in range(BATCH_TILES):
                 pass_words = words_in[:, s, m, first_word : first_word + words_per_pass].rearrange(
                     "b (p u) -> b u p", u=2
@@ -160,58 +138,42 @@ def tile_multidimensinalgrucell_pb_kernel(
                     nc.tensor.transpose(turned[:, m, u, :], pass_words[:, u, :], ident_f32[:])
             q_grouped = q_stage.tile([P, BATCH * PACK], BF16, align_bytes=64)
             side_by_side = q_grouped[:].bitcast(F32).rearrange("p (m b u) -> p m b u", m=BATCH_TILES, u=2)
-            if g % 2 == 0:
-                nc.vector.tensor_copy(out=side_by_side, in_=turned[:].rearrange("p m u b -> p m b u"))
-            else:
-                nc.scalar.copy(out=side_by_side, in_=turned[:].rearrange("p m u b -> p m b u"))
+            nc.scalar.copy(out=side_by_side, in_=turned[:].rearrange("p m u b -> p m b u"))
             q_grouped_of[g] = q_grouped
-            if g >= 1:
-                quantise_q(g - 1)
-        quantise_q(PASSES - 1)
 
-        kept_codes = keep.tile([P, WIDE_PASSES * GATES, ROUND_UNITS], U32, align_bytes=64)
-        kept_scales = keep.tile([P, WIDE_PASSES * GATES, ROUND_UNITS], U8, align_bytes=64)
         grouped_of = {}
         codes_of = {}
         sums = {}
 
-        def is_kept(piece):
-            g, gate, r = piece
-            return r == 1 and g < WIDE_PASSES
-
-        def regroup(piece, vector_cols):
-            raw = raw_of[piece]
+        def regroup(c):
+            r = c // CHUNKS_PER_ROUND
+            split = VECTOR_COLS_FIRST_ROUND if r == 0 else VECTOR_COLS_LATER_ROUNDS
+            raw = raw_of[c]
             grouped = grouped_pool.tile([P, ROUND_UNITS, PACK], BF16, align_bytes=64)
             nc.vector.tensor_copy(
-                out=grouped[:, 0:vector_cols, :].rearrange("p (c i) t -> p c t i", i=4),
-                in_=raw[:, :, 0:vector_cols].rearrange("p t (c i) -> p c t i", i=4),
+                out=grouped[:, 0:split, :].rearrange("p (c i) t -> p c t i", i=4),
+                in_=raw[:, :, 0:split].rearrange("p t (c i) -> p c t i", i=4),
             )
             nc.scalar.copy(
-                out=grouped[:, vector_cols:ROUND_UNITS, :].rearrange("p (c i) t -> p c t i", i=4),
-                in_=raw[:, :, vector_cols:ROUND_UNITS].rearrange("p t (c i) -> p c t i", i=4),
+                out=grouped[:, split:ROUND_UNITS, :].rearrange("p (c i) t -> p c t i", i=4),
+                in_=raw[:, :, split:ROUND_UNITS].rearrange("p t (c i) -> p c t i", i=4),
             )
-            grouped_of[piece] = grouped
+            grouped_of[c] = grouped
 
-        def quantise(piece):
-            g, gate, r = piece
-            if is_kept(piece):
-                w_codes = kept_codes[:, g * GATES + gate, :]
-                w_scales = kept_scales[:, g * GATES + gate, :]
-            else:
-                codes_tile = code_pool.tile([P, ROUND_UNITS], U32, align_bytes=64)
-                scales_tile = code_pool.tile([P, ROUND_UNITS], U8, align_bytes=64)
-                w_codes = codes_tile[:]
-                w_scales = scales_tile[:]
+        def quantise(c):
+            w_codes = code_pool.tile([P, ROUND_UNITS], U32, align_bytes=64)
+            w_scales = code_pool.tile([P, ROUND_UNITS], U8, align_bytes=64)
             nc.vector.quantize_mx(
-                out=w_codes.bitcast(FP8X4),
-                scales=w_scales,
-                in_=grouped_of[piece][:].rearrange("p w t -> p (w t)"),
+                out=w_codes[:].bitcast(FP8X4),
+                scales=w_scales[:],
+                in_=grouped_of[c][:].rearrange("p w t -> p (w t)"),
             )
-            codes_of[piece] = (w_codes, w_scales)
+            codes_of[c] = (w_codes, w_scales)
 
-        def multiply(piece):
-            g, gate, r = piece
-            w_codes, w_scales = codes_of[piece]
+        def multiply(c):
+            gate = c % GATES
+            g = (c // GATES) % PASSES
+            w_codes, w_scales = codes_of[c]
             for m in range(BATCH_TILES):
                 if g == 0:
                     sums[(m, gate)] = bank([P, ROUND_UNITS], F32, m * GATES + gate)
@@ -220,8 +182,8 @@ def tile_multidimensinalgrucell_pb_kernel(
                     out=sums[(m, gate)][:],
                     lhsT=q_codes[:, g, rows].bitcast(FP8X4),
                     lhsT_scale=q_scales[:, g, rows],
-                    rhs=w_codes.bitcast(FP8X4),
-                    rhs_scale=w_scales,
+                    rhs=w_codes[:].bitcast(FP8X4),
+                    rhs_scale=w_scales[:],
                     start=(g == 0),
                     stop=(g == PASSES - 1),
                 )
@@ -244,47 +206,78 @@ def tile_multidimensinalgrucell_pb_kernel(
                         op=ALU.add,
                     )
 
-            def subtract_max(m):
-                pair_max = scratch.tile([P, 2, ROUND_UNITS], F32, name="pair")
-                top = scratch.tile([P, ROUND_UNITS], F32, name="top")
-                nc.vector.tensor_tensor(
-                    out=pair_max[:], in0=logits[m][:, 0:2, :], in1=logits[m][:, 2:4, :], op=ALU.max
-                )
-                nc.vector.tensor_tensor(
-                    out=top[:], in0=pair_max[:, 0, :], in1=pair_max[:, 1, :], op=ALU.max
-                )
-                nc.vector.tensor_tensor(
-                    out=logits[m][:],
-                    in0=logits[m][:],
-                    in1=top[:].unsqueeze(1).to_broadcast([P, GATES, ROUND_UNITS]),
-                    op=ALU.subtract,
-                )
+            pair_max = {}
+            top = {}
+            pair_below = {}
+            weighted = {}
+            pair_above = {}
 
-            def exponentials(m):
-                weight[m] = per_tile.tile([P, GATES, ROUND_UNITS], F32, name="weight")
-                nc.scalar.activation(out=weight[m][:], in_=logits[m][:], func=ACT.Exp)
+            def maxima():
+                for m in range(BATCH_TILES):
+                    pair_max[m] = per_tile.tile([P, 2, ROUND_UNITS], F32, name="pair_max")
+                    nc.vector.tensor_tensor(
+                        out=pair_max[m][:], in0=logits[m][:, 0:2, :], in1=logits[m][:, 2:4, :], op=ALU.max
+                    )
+                for m in range(BATCH_TILES):
+                    top[m] = per_tile.tile([P, ROUND_UNITS], F32, name="top")
+                    nc.vector.tensor_tensor(
+                        out=top[m][:], in0=pair_max[m][:, 0, :], in1=pair_max[m][:, 1, :], op=ALU.max
+                    )
 
-            def add_gates(total, terms):
-                pair_sum = scratch.tile([P, 2, ROUND_UNITS], F32, name="pair")
+            def subtract_maxima():
+                for m in range(BATCH_TILES):
+                    nc.vector.tensor_tensor(
+                        out=logits[m][:],
+                        in0=logits[m][:],
+                        in1=top[m][:].unsqueeze(1).to_broadcast([P, GATES, ROUND_UNITS]),
+                        op=ALU.subtract,
+                    )
+
+            def exponentials():
+                for m in range(BATCH_TILES):
+                    weight[m] = per_tile.tile([P, GATES, ROUND_UNITS], F32, name="weight")
+                    nc.scalar.activation(out=weight[m][:], in_=logits[m][:], func=ACT.Exp)
+
+            def add_pairs(pair_sum, terms):
                 nc.vector.tensor_tensor(
                     out=pair_sum[:], in0=terms[:, 0:2, :], in1=terms[:, 2:4, :], op=ALU.add
                 )
+
+            def add_halves(total, pair_sum):
                 nc.vector.tensor_tensor(
                     out=total, in0=pair_sum[:, 0, :], in1=pair_sum[:, 1, :], op=ALU.add
                 )
 
-            def denominator(m):
-                add_gates(below[:, m, :], weight[m])
-
-            def numerator(m):
+            def weigh(m):
+                weighted[m] = per_tile.tile([P, GATES, ROUND_UNITS], F32, name="weighted")
                 nc.vector.tensor_tensor(
-                    out=weight[m][:], in0=weight[m][:], in1=rows_in[:, 0:GATES, m, cols], op=ALU.mult
+                    out=weighted[m][:], in0=weight[m][:], in1=rows_in[:, 0:GATES, m, cols], op=ALU.mult
                 )
-                add_gates(above[:, m, :], weight[m])
 
-            def reciprocal():
+            def denominators():
+                for m in range(BATCH_TILES):
+                    pair_below[m] = per_tile.tile([P, 2, ROUND_UNITS], F32, name="pair_sum")
+                add_pairs(pair_below[0], weight[0])
+                weigh(0)
+                add_pairs(pair_below[1], weight[1])
+                for m in range(BATCH_TILES):
+                    add_halves(below[:, m, :], pair_below[m])
+
+            def reciprocals():
                 nc.scalar.activation(out=below[:], in_=below[:], func=ACT.Ln)
                 nc.scalar.activation(out=below[:], in_=below[:], func=ACT.Exp, scale=-1.0)
+
+            def numerators():
+                weigh(1)
+                for m in range(BATCH_TILES):
+                    pair_above[m] = per_tile.tile([P, 2, ROUND_UNITS], F32, name="pair_sum")
+                    add_pairs(pair_above[m], weighted[m])
+                for m in range(BATCH_TILES):
+                    add_halves(above[:, m, :], pair_above[m])
+
+            def reciprocals_and_numerators():
+                reciprocals()
+                numerators()
 
             def divide_and_store():
                 for m in range(BATCH_TILES):
@@ -293,46 +286,36 @@ def tile_multidimensinalgrucell_pb_kernel(
                     )
                     nc.sync.dma_start(out=out[m * P : (m + 1) * P, cols], in_=above[:, m, :])
 
-            def step_1():
-                subtract_max(0)
-
-            def step_2():
-                exponentials(0)
-                subtract_max(1)
-
-            def step_3():
-                exponentials(1)
-                denominator(0)
-                numerator(0)
-
-            def step_4():
-                denominator(1)
-
-            def step_5():
-                reciprocal()
-                numerator(1)
-
-            return [step_1, step_2, step_3, step_4, step_5, divide_and_store]
+            return [
+                maxima,
+                subtract_maxima,
+                exponentials,
+                denominators,
+                reciprocals_and_numerators,
+                divide_and_store,
+            ]
 
         steps = []
-        for c in range(len(pieces) + 2):
-            if c + PREFETCH < len(pieces):
-                load_for(pieces[c + PREFETCH])
-            if c + PREFETCH == first_round_pieces:
+        multiplied = 0
+        for c in range(CHUNKS + 2):
+            if c + PREFETCH < CHUNKS:
+                load_chunk(c + PREFETCH)
+            if c + PREFETCH == CHUNKS_PER_ROUND:
                 load_row_set(0)
-            if c < len(pieces):
-                regroup(pieces[c], VECTOR_COLS_BESIDE_SOFTMAX if steps else VECTOR_COLS)
-            if 1 <= c <= len(pieces):
-                quantise(pieces[c - 1])
-            if c >= 2 and not is_kept(pieces[c - 2]):
-                multiply(pieces[c - 2])
-            if c - 2 == first_round_pieces - 1:
-                steps = softmax_and_blend(0)
-                for piece in pieces[0:first_round_pieces]:
-                    if is_kept(piece):
-                        multiply(piece)
-            if c - 2 == len(pieces) - 1:
-                steps = softmax_and_blend(1)
+            if c < CHUNKS:
+                regroup(c)
+            if 1 <= c <= CHUNKS:
+                quantise(c - 1)
+            if c < PASSES:
+                turn_q(c)
+            if 1 <= c <= PASSES:
+                quantise_q(c - 1)
+            if c > PASSES:
+                for ready in range(multiplied, c - 1):
+                    multiply(ready)
+                    if ready % CHUNKS_PER_ROUND == CHUNKS_PER_ROUND - 1:
+                        steps = softmax_and_blend(ready // CHUNKS_PER_ROUND)
+                multiplied = c - 1
             if steps and c % STEP_EVERY == 0:
                 steps[0]()
                 steps = steps[1:]

@@ -19,19 +19,24 @@ BATCH = 256
 UNITS = 1024
 K_ALL = 4 * UNITS
 GATES = 4
+LAST = GATES - 1
 BATCH_TILES = BATCH // P
 PASSES = K_ALL // K_PASS
-ROUND_UNITS = 512
-ROUNDS = UNITS // ROUND_UNITS
-CHUNKS_PER_ROUND = PASSES * GATES
-CHUNKS = ROUNDS * CHUNKS_PER_ROUND
+HALF = 512
+HALVES = UNITS // HALF
+BANKS = 8
 
 FLOPS = 2 * BATCH * K_ALL * GATES * UNITS
 
-VECTOR_COLS_FIRST_ROUND = 240
-VECTOR_COLS_LATER_ROUNDS = 176
-PREFETCH = 8
-STEP_EVERY = 4
+BLOCKS = [
+    (0, 0, UNITS, 0.50),
+    (1, 0, UNITS, 0.46),
+    (2, 0, UNITS, 0.44),
+    (3, 0, HALF, 0.10),
+    (3, HALF, HALF, 0.35),
+]
+CHUNKS = [(b, g) for b in range(len(BLOCKS)) for g in range(PASSES)]
+PREFETCH = 5
 
 
 def tile_multidimensinalgrucell_pb_kernel(
@@ -48,9 +53,8 @@ def tile_multidimensinalgrucell_pb_kernel(
         keep = stack.enter_context(tc.tile_pool(name="keep", bufs=1))
         q_stage = stack.enter_context(tc.tile_pool(name="q_stage", bufs=2))
         raw_pool = stack.enter_context(tc.tile_pool(name="raw", bufs=PREFETCH + 2))
-        grouped_pool = stack.enter_context(tc.tile_pool(name="grouped", bufs=6))
-        code_pool = stack.enter_context(tc.tile_pool(name="codes", bufs=PASSES + 4))
-        per_tile = stack.enter_context(tc.tile_pool(name="per_tile", bufs=2))
+        grouped_pool = stack.enter_context(tc.tile_pool(name="grouped", bufs=4))
+        code_pool = stack.enter_context(tc.tile_pool(name="codes", bufs=4))
         scratch = stack.enter_context(tc.tile_pool(name="scratch", bufs=1))
         psum = stack.enter_context(tc.psum_pool(name="psum", bufs=1))
 
@@ -62,11 +66,6 @@ def tile_multidimensinalgrucell_pb_kernel(
         ident_bf16 = keep.tile([P, P], BF16)
         make_identity(nc, ident_bf16[:])
 
-        bias_rows = keep.tile([P, UNITS], BF16)
-        nc.vector.memset(bias_rows[:].bitcast(I32), 0)
-        for gate in range(GATES):
-            nc.sync.dma_start(out=bias_rows[gate : gate + 1, :], in_=biases[gate].unsqueeze(0))
-
         rows_in = keep.tile([P, len(row_sets), BATCH_TILES, UNITS], BF16)
 
         def load_row_set(s):
@@ -76,36 +75,48 @@ def tile_multidimensinalgrucell_pb_kernel(
 
         raw_of = {}
 
-        def load_chunk(c):
-            gate = c % GATES
-            g = (c // GATES) % PASSES
-            r = c // CHUNKS_PER_ROUND
-            raw = raw_pool.tile([P, PACK, ROUND_UNITS], BF16)
-            nc.sync.dma_start(
-                out=raw[:],
-                in_=weights[gate][
-                    g * K_PASS : (g + 1) * K_PASS, r * ROUND_UNITS : (r + 1) * ROUND_UNITS
-                ].rearrange("(p t) w -> p t w", t=PACK),
-            )
+        def load_chunk(c, pieces=1):
+            b, g = CHUNKS[c]
+            gate, first, width, share = BLOCKS[b]
+            raw = raw_pool.tile([P, PACK, width], BF16, name="raw")
+            rows = weights[gate][g * K_PASS : (g + 1) * K_PASS, :].rearrange("(p t) w -> p t w", t=PACK)
+            piece = width // pieces
+            for i in range(pieces):
+                nc.sync.dma_start(
+                    out=raw[:, :, i * piece : (i + 1) * piece],
+                    in_=rows[:, :, first + i * piece : first + (i + 1) * piece],
+                )
             raw_of[c] = raw
 
-        for c in range(PREFETCH):
-            load_chunk(c)
-            if c + 1 < len(row_sets):
-                load_row_set(c + 1)
+        bias_rows = keep.tile([P, UNITS], BF16)
+        nc.vector.memset(bias_rows[:].bitcast(I32), 0)
 
-        pick = keep.tile([P, GATES], BF16)
+        load_chunk(0, pieces=2)
+        load_row_set(1)
+        load_chunk(1)
+        for gate in range(GATES):
+            nc.sync.dma_start(out=bias_rows[gate : gate + 1, :], in_=biases[gate].unsqueeze(0))
+        load_row_set(2)
+        load_chunk(2)
+        load_row_set(3)
+        load_chunk(3)
+        load_row_set(4)
+        for c in range(4, PREFETCH):
+            load_chunk(c)
+
+        pick = keep.tile([P, LAST], BF16)
         nc.vector.tensor_tensor(
             out=pick[:],
-            in0=ident_bf16[:, 0:GATES],
-            in1=ident_bf16[:, 0:1].to_broadcast([P, GATES]),
+            in0=ident_bf16[:, 0:LAST],
+            in1=ident_bf16[:, LAST : LAST + 1].to_broadcast([P, LAST]),
             op=ALU.subtract,
         )
-        bias_gap = keep.tile([P, GATES - 1, UNITS], F32)
-        for gate in range(1, GATES):
-            for r in range(ROUNDS):
-                cols = slice(r * ROUND_UNITS, (r + 1) * ROUND_UNITS)
-                spread = bank([P, ROUND_UNITS], F32, (gate - 1) * ROUNDS + r)
+        bias_gap = keep.tile([P, LAST, UNITS], F32)
+
+        def spread_bias(gate):
+            for h in range(HALVES):
+                cols = slice(h * HALF, (h + 1) * HALF)
+                spread = bank([P, HALF], F32, 4 + (gate * HALVES + h) % 4)
                 nc.tensor.matmul(
                     out=spread[:],
                     lhsT=pick[:, gate : gate + 1].to_broadcast([P, P]),
@@ -113,7 +124,7 @@ def tile_multidimensinalgrucell_pb_kernel(
                     start=True,
                     stop=True,
                 )
-                nc.scalar.copy(out=bias_gap[:, gate - 1, cols], in_=spread[:])
+                nc.scalar.copy(out=bias_gap[:, gate, cols], in_=spread[:])
 
         q_codes = keep.tile([P, PASSES, BATCH], U32, align_bytes=64)
         q_scales = keep.tile([P, PASSES, BATCH], U8, align_bytes=64)
@@ -129,7 +140,7 @@ def tile_multidimensinalgrucell_pb_kernel(
         def turn_q(g):
             s = 1 + (g * K_PASS) // UNITS
             first_word = ((g * K_PASS) % UNITS) // 2
-            turned = bank([P, BATCH_TILES, 2, P], F32, (g + 6) % 8)
+            turned = bank([P, BATCH_TILES, 2, P], F32, 4 + g % 4)
             for m in range(BATCH_TILES):
                 pass_words = words_in[:, s, m, first_word : first_word + words_per_pass].rearrange(
                     "b (p u) -> b u p", u=2
@@ -145,24 +156,30 @@ def tile_multidimensinalgrucell_pb_kernel(
         codes_of = {}
         sums = {}
 
-        def regroup(c):
-            r = c // CHUNKS_PER_ROUND
-            split = VECTOR_COLS_FIRST_ROUND if r == 0 else VECTOR_COLS_LATER_ROUNDS
+        def regroup(c, pieces=1):
+            b, g = CHUNKS[c]
+            gate, first, width, share = BLOCKS[b]
             raw = raw_of[c]
-            grouped = grouped_pool.tile([P, ROUND_UNITS, PACK], BF16, align_bytes=64)
-            nc.vector.tensor_copy(
-                out=grouped[:, 0:split, :].rearrange("p (c i) t -> p c t i", i=4),
-                in_=raw[:, :, 0:split].rearrange("p t (c i) -> p c t i", i=4),
-            )
-            nc.scalar.copy(
-                out=grouped[:, split:ROUND_UNITS, :].rearrange("p (c i) t -> p c t i", i=4),
-                in_=raw[:, :, split:ROUND_UNITS].rearrange("p t (c i) -> p c t i", i=4),
-            )
+            grouped = grouped_pool.tile([P, width, PACK], BF16, align_bytes=64, name="grouped")
+            piece = width // pieces
+            mine = int(piece * share) // 8 * 8
+            for i in range(pieces):
+                lo, mid, hi = i * piece, i * piece + mine, (i + 1) * piece
+                nc.vector.tensor_copy(
+                    out=grouped[:, lo:mid, :].rearrange("p (c i) t -> p c t i", i=4),
+                    in_=raw[:, :, lo:mid].rearrange("p t (c i) -> p c t i", i=4),
+                )
+                nc.scalar.copy(
+                    out=grouped[:, mid:hi, :].rearrange("p (c i) t -> p c t i", i=4),
+                    in_=raw[:, :, mid:hi].rearrange("p t (c i) -> p c t i", i=4),
+                )
             grouped_of[c] = grouped
 
         def quantise(c):
-            w_codes = code_pool.tile([P, ROUND_UNITS], U32, align_bytes=64)
-            w_scales = code_pool.tile([P, ROUND_UNITS], U8, align_bytes=64)
+            b, g = CHUNKS[c]
+            width = BLOCKS[b][2]
+            w_codes = code_pool.tile([P, width], U32, align_bytes=64, name="w_codes")
+            w_scales = code_pool.tile([P, width], U8, align_bytes=64, name="w_scales")
             nc.vector.quantize_mx(
                 out=w_codes[:].bitcast(FP8X4),
                 scales=w_scales[:],
@@ -170,154 +187,187 @@ def tile_multidimensinalgrucell_pb_kernel(
             )
             codes_of[c] = (w_codes, w_scales)
 
+        next_bank = [0]
+
         def multiply(c):
-            gate = c % GATES
-            g = (c // GATES) % PASSES
+            b, g = CHUNKS[c]
+            gate, first, width, share = BLOCKS[b]
             w_codes, w_scales = codes_of[c]
             for m in range(BATCH_TILES):
-                if g == 0:
-                    sums[(m, gate)] = bank([P, ROUND_UNITS], F32, m * GATES + gate)
                 rows = slice(m * P, (m + 1) * P)
-                nc.tensor.matmul_mx(
-                    out=sums[(m, gate)][:],
-                    lhsT=q_codes[:, g, rows].bitcast(FP8X4),
-                    lhsT_scale=q_scales[:, g, rows],
-                    rhs=w_codes[:].bitcast(FP8X4),
-                    rhs_scale=w_scales[:],
-                    start=(g == 0),
-                    stop=(g == PASSES - 1),
-                )
+                for i in range(width // HALF):
+                    h = first // HALF + i
+                    cols = slice(i * HALF, (i + 1) * HALF)
+                    if g == 0:
+                        sums[(gate, h, m)] = bank([P, HALF], F32, next_bank[0] % BANKS)
+                        next_bank[0] += 1
+                    nc.tensor.matmul_mx(
+                        out=sums[(gate, h, m)][:],
+                        lhsT=q_codes[:, g, rows].bitcast(FP8X4),
+                        lhsT_scale=q_scales[:, g, rows],
+                        rhs=w_codes[:, cols].bitcast(FP8X4),
+                        rhs_scale=w_scales[:, cols],
+                        start=(g == 0),
+                        stop=(g == PASSES - 1),
+                    )
 
-        def softmax_and_blend(r):
-            cols = slice(r * ROUND_UNITS, (r + 1) * ROUND_UNITS)
-            logits = {}
-            weight = {}
-            below = scratch.tile([P, BATCH_TILES, ROUND_UNITS], F32, name="below")
-            above = scratch.tile([P, BATCH_TILES, ROUND_UNITS], F32, name="above")
+        tensor_tensor = nc.vector.tensor_tensor
+        shape = [P, BATCH_TILES, HALF]
+        logits = {}
+        peak = {}
+        total = {}
+        mean = {}
+        gap = {}
+        lean = {}
 
+        for h in range(HALVES):
+            logits[h] = keep.tile([P, LAST, BATCH_TILES, HALF], F32, name="logits%d" % h)
+            peak[h] = keep.tile(shape, F32, name="peak%d" % h)
+
+        def add_bias(gate, h):
+            cols = slice(h * HALF, (h + 1) * HALF)
             for m in range(BATCH_TILES):
-                logits[m] = per_tile.tile([P, GATES, ROUND_UNITS], F32, name="logits")
-                nc.scalar.copy(out=logits[m][:, 0, :], in_=sums[(m, 0)][:])
-                for gate in range(1, GATES):
-                    nc.vector.tensor_tensor(
-                        out=logits[m][:, gate, :],
-                        in0=sums[(m, gate)][:],
-                        in1=bias_gap[:, gate - 1, cols],
-                        op=ALU.add,
-                    )
-
-            pair_max = {}
-            top = {}
-            pair_below = {}
-            weighted = {}
-            pair_above = {}
-
-            def maxima():
-                for m in range(BATCH_TILES):
-                    pair_max[m] = per_tile.tile([P, 2, ROUND_UNITS], F32, name="pair_max")
-                    nc.vector.tensor_tensor(
-                        out=pair_max[m][:], in0=logits[m][:, 0:2, :], in1=logits[m][:, 2:4, :], op=ALU.max
-                    )
-                for m in range(BATCH_TILES):
-                    top[m] = per_tile.tile([P, ROUND_UNITS], F32, name="top")
-                    nc.vector.tensor_tensor(
-                        out=top[m][:], in0=pair_max[m][:, 0, :], in1=pair_max[m][:, 1, :], op=ALU.max
-                    )
-
-            def subtract_maxima():
-                for m in range(BATCH_TILES):
-                    nc.vector.tensor_tensor(
-                        out=logits[m][:],
-                        in0=logits[m][:],
-                        in1=top[m][:].unsqueeze(1).to_broadcast([P, GATES, ROUND_UNITS]),
-                        op=ALU.subtract,
-                    )
-
-            def exponentials():
-                for m in range(BATCH_TILES):
-                    weight[m] = per_tile.tile([P, GATES, ROUND_UNITS], F32, name="weight")
-                    nc.scalar.activation(out=weight[m][:], in_=logits[m][:], func=ACT.Exp)
-
-            def add_pairs(pair_sum, terms):
-                nc.vector.tensor_tensor(
-                    out=pair_sum[:], in0=terms[:, 0:2, :], in1=terms[:, 2:4, :], op=ALU.add
+                tensor_tensor(
+                    out=logits[h][:, gate, m, :],
+                    in0=sums[(gate, h, m)][:],
+                    in1=bias_gap[:, gate, cols],
+                    op=ALU.add,
                 )
 
-            def add_halves(total, pair_sum):
-                nc.vector.tensor_tensor(
-                    out=total, in0=pair_sum[:, 0, :], in1=pair_sum[:, 1, :], op=ALU.add
+        def peak_two(h):
+            tensor_tensor(out=peak[h][:], in0=logits[h][:, 0, :, :], in1=logits[h][:, 1, :, :], op=ALU.max)
+
+        def peak_three(h):
+            tensor_tensor(out=peak[h][:], in0=peak[h][:], in1=logits[h][:, 2, :, :], op=ALU.max)
+
+        def subtract_peak(h):
+            for gate in range(LAST):
+                tensor_tensor(
+                    out=logits[h][:, gate, :, :], in0=logits[h][:, gate, :, :], in1=peak[h][:], op=ALU.subtract
                 )
 
-            def weigh(m):
-                weighted[m] = per_tile.tile([P, GATES, ROUND_UNITS], F32, name="weighted")
-                nc.vector.tensor_tensor(
-                    out=weighted[m][:], in0=weight[m][:], in1=rows_in[:, 0:GATES, m, cols], op=ALU.mult
+        def exponentials(h):
+            for gate in range(LAST):
+                nc.scalar.activation(out=logits[h][:, gate, :, :], in_=logits[h][:, gate, :, :], func=ACT.Exp)
+
+        def weigh(h):
+            cols = slice(h * HALF, (h + 1) * HALF)
+            weighted[h] = scratch.tile([P, LAST, BATCH_TILES, HALF], F32, name="weighted%d" % h)
+            for gate in range(LAST):
+                tensor_tensor(
+                    out=weighted[h][:, gate, :, :],
+                    in0=logits[h][:, gate, :, :],
+                    in1=rows_in[:, gate, :, cols],
+                    op=ALU.mult,
                 )
 
-            def denominators():
-                for m in range(BATCH_TILES):
-                    pair_below[m] = per_tile.tile([P, 2, ROUND_UNITS], F32, name="pair_sum")
-                add_pairs(pair_below[0], weight[0])
-                weigh(0)
-                add_pairs(pair_below[1], weight[1])
-                for m in range(BATCH_TILES):
-                    add_halves(below[:, m, :], pair_below[m])
+        weighted = {}
 
-            def reciprocals():
-                nc.scalar.activation(out=below[:], in_=below[:], func=ACT.Ln)
-                nc.scalar.activation(out=below[:], in_=below[:], func=ACT.Exp, scale=-1.0)
+        def add_two(h):
+            total[h] = scratch.tile(shape, F32, name="total%d" % h)
+            tensor_tensor(out=total[h][:], in0=logits[h][:, 0, :, :], in1=logits[h][:, 1, :, :], op=ALU.add)
 
-            def numerators():
-                weigh(1)
-                for m in range(BATCH_TILES):
-                    pair_above[m] = per_tile.tile([P, 2, ROUND_UNITS], F32, name="pair_sum")
-                    add_pairs(pair_above[m], weighted[m])
-                for m in range(BATCH_TILES):
-                    add_halves(above[:, m, :], pair_above[m])
+        def add_three(h):
+            tensor_tensor(out=total[h][:], in0=total[h][:], in1=logits[h][:, 2, :, :], op=ALU.add)
 
-            def reciprocals_and_numerators():
-                reciprocals()
-                numerators()
+        def logarithm(h):
+            gap[h] = scratch.tile(shape, F32, name="log_total%d" % h)
+            nc.scalar.activation(out=gap[h][:], in_=total[h][:], func=ACT.Ln)
 
-            def divide_and_store():
-                for m in range(BATCH_TILES):
-                    nc.vector.tensor_tensor(
-                        out=above[:, m, :], in0=above[:, m, :], in1=below[:, m, :], op=ALU.mult
-                    )
-                    nc.sync.dma_start(out=out[m * P : (m + 1) * P, cols], in_=above[:, m, :])
+        def one_over_total(h):
+            nc.scalar.activation(out=total[h][:], in_=gap[h][:], func=ACT.Exp, scale=-1.0)
 
-            return [
-                maxima,
-                subtract_maxima,
-                exponentials,
-                denominators,
-                reciprocals_and_numerators,
-                divide_and_store,
-            ]
+        def blend_two(h):
+            mean[h] = weighted[h][:, 0, :, :]
+            lean[h] = weighted[h][:, 1, :, :]
+            tensor_tensor(out=mean[h], in0=mean[h], in1=lean[h], op=ALU.add)
 
-        steps = []
-        multiplied = 0
-        for c in range(CHUNKS + 2):
-            if c + PREFETCH < CHUNKS:
+        def blend_three(h):
+            tensor_tensor(out=mean[h], in0=mean[h], in1=weighted[h][:, 2, :, :], op=ALU.add)
+
+        def minus_lse(h):
+            nc.vector.scalar_tensor_tensor(
+                out=gap[h][:], in0=peak[h][:], scalar=-1.0, in1=gap[h][:], op0=ALU.mult, op1=ALU.subtract
+            )
+
+        def divide(h):
+            tensor_tensor(out=mean[h], in0=mean[h], in1=total[h][:], op=ALU.mult)
+
+        def distance(h):
+            cols = slice(h * HALF, (h + 1) * HALF)
+            tensor_tensor(out=lean[h], in0=rows_in[:, LAST, :, cols], in1=mean[h], op=ALU.subtract)
+
+        def last_gate(h):
+            for m in range(BATCH_TILES):
+                tensor_tensor(
+                    out=gap[h][:, m, :], in0=sums[(LAST, h, m)][:], in1=gap[h][:, m, :], op=ALU.add
+                )
+                nc.scalar.activation(out=gap[h][:, m, :], in_=gap[h][:, m, :], func=ACT.Tanh, scale=0.5)
+
+        def join_and_store(h):
+            cols = slice(h * HALF, (h + 1) * HALF)
+            for m in range(BATCH_TILES):
+                nc.vector.scalar_tensor_tensor(
+                    out=lean[h][:, m, :], in0=gap[h][:, m, :], scalar=1.0, in1=lean[h][:, m, :],
+                    op0=ALU.add, op1=ALU.mult,
+                )
+            for m in range(BATCH_TILES):
+                nc.vector.scalar_tensor_tensor(
+                    out=mean[h][:, m, :], in0=lean[h][:, m, :], scalar=0.5, in1=mean[h][:, m, :],
+                    op0=ALU.mult, op1=ALU.add,
+                )
+                nc.sync.dma_start(out=out[m * P : (m + 1) * P, cols], in_=mean[h][:, m, :])
+
+        plan = {}
+
+        def at(turn, fn, *args):
+            plan.setdefault(turn, []).append((fn, args))
+
+        end = {b: (b + 1) * PASSES + 2 for b in range(len(BLOCKS))}
+        for h in range(HALVES):
+            at(end[0] + h, add_bias, 0, h)
+            at(end[1] + h, add_bias, 1, h)
+            at(end[1] + 2 + h, peak_two, h)
+            at(end[2], add_bias, 2, h)
+        for h in range(HALVES):
+            t = end[2] + 1 + h
+            at(t, peak_three, h)
+            at(t + 1, subtract_peak, h)
+            at(t + 1, exponentials, h)
+            at(t + 2, add_two, h)
+            at(t + 2, weigh, h)
+            at(t + 3, add_three, h)
+        for h in range(HALVES):
+            at(end[2] + 5, logarithm, h)
+        for h in range(HALVES):
+            at(end[2] + 5, one_over_total, h)
+        for h in range(HALVES):
+            at(end[2] + 5, blend_two, h)
+            at(end[2] + 6, blend_three, h)
+            at(end[2] + 6, minus_lse, h)
+            at(end[2] + 7, divide, h)
+            at(end[2] + 8 + h, distance, h)
+            t = end[3 + h]
+            at(t + 1 - h, last_gate, h)
+            at(t + 2 - h, join_and_store, h)
+
+        count = len(CHUNKS)
+        for c in range(max(max(plan) + 1, count + 2)):
+            if c + PREFETCH < count:
                 load_chunk(c + PREFETCH)
-            if c + PREFETCH == CHUNKS_PER_ROUND:
+            if c == PASSES:
                 load_row_set(0)
-            if c < CHUNKS:
-                regroup(c)
-            if 1 <= c <= CHUNKS:
-                quantise(c - 1)
+            if c < count:
+                regroup(c, pieces=2 if c == 0 else 1)
             if c < PASSES:
                 turn_q(c)
+            if 2 <= c < 2 + LAST:
+                spread_bias(c - 2)
+            if 1 <= c <= count:
+                quantise(c - 1)
             if 1 <= c <= PASSES:
                 quantise_q(c - 1)
-            if c > PASSES:
-                for ready in range(multiplied, c - 1):
-                    multiply(ready)
-                    if ready % CHUNKS_PER_ROUND == CHUNKS_PER_ROUND - 1:
-                        steps = softmax_and_blend(ready // CHUNKS_PER_ROUND)
-                multiplied = c - 1
-            if steps and c % STEP_EVERY == 0:
-                steps[0]()
-                steps = steps[1:]
-        for step in steps:
-            step()
+            if 2 <= c < count + 2:
+                multiply(c - 2)
+            for fn, args in plan.get(c, []):
+                fn(*args)

@@ -29,14 +29,25 @@ BANKS = 8
 FLOPS = 2 * BATCH * K_ALL * GATES * UNITS
 
 BLOCKS = [
-    (0, 0, UNITS, 0.50),
-    (1, 0, UNITS, 0.46),
-    (2, 0, UNITS, 0.44),
-    (3, 0, HALF, 0.10),
-    (3, HALF, HALF, 0.35),
+    (0, 0, UNITS, 0.60),
+    (1, 0, UNITS, 0.52),
+    (2, 0, UNITS, 0.42),
+    (3, 0, HALF, 0.42),
+    (3, HALF, HALF, 0.28),
 ]
-CHUNKS = [(b, g) for b in range(len(BLOCKS)) for g in range(PASSES)]
 PREFETCH = 5
+LAST_PIECES = 2
+FIRST_PIECES = 2
+Q_LAG = 2
+
+
+def units_of(blocks):
+    units = []
+    for b, (gate, first, width, share) in enumerate(blocks):
+        span = UNITS // width
+        for g in range(0, PASSES, span):
+            units.append((b, [(g + i, first, width) for i in range(span)]))
+    return units
 
 
 def tile_multidimensinalgrucell_pb_kernel(
@@ -47,6 +58,7 @@ def tile_multidimensinalgrucell_pb_kernel(
     weights = [w_zi, w_zl, w_zt, w_zd]
     biases = [b_zi, b_zl, b_zt, b_zd]
     row_sets = [h_cand, left_state, top_state, diagonal_state, x]
+    units = units_of(BLOCKS)
 
     with ExitStack() as stack:
         stack.enter_context(tc.manual_schedule())
@@ -75,34 +87,36 @@ def tile_multidimensinalgrucell_pb_kernel(
 
         raw_of = {}
 
-        def load_chunk(c, pieces=1):
-            b, g = CHUNKS[c]
-            gate, first, width, share = BLOCKS[b]
-            raw = raw_pool.tile([P, PACK, width], BF16, name="raw")
-            rows = weights[gate][g * K_PASS : (g + 1) * K_PASS, :].rearrange("(p t) w -> p t w", t=PACK)
-            piece = width // pieces
-            for i in range(pieces):
-                nc.sync.dma_start(
-                    out=raw[:, :, i * piece : (i + 1) * piece],
-                    in_=rows[:, :, first + i * piece : first + (i + 1) * piece],
-                )
-            raw_of[c] = raw
+        def load_unit(c, pieces=1):
+            b, parts = units[c]
+            gate = BLOCKS[b][0]
+            raw = raw_pool.tile([P, PACK * UNITS], BF16, name="raw")
+            raw_of[c] = []
+            start = 0
+            for g, first, width in parts:
+                part = raw[:, start * PACK : (start + width) * PACK].rearrange("p (t w) -> p t w", t=PACK)
+                rows = weights[gate][g * K_PASS : (g + 1) * K_PASS, :].rearrange("(p t) w -> p t w", t=PACK)
+                piece = width // pieces
+                for i in range(pieces):
+                    nc.sync.dma_start(
+                        out=part[:, :, i * piece : (i + 1) * piece],
+                        in_=rows[:, :, first + i * piece : first + (i + 1) * piece],
+                    )
+                raw_of[c].append((start, width, part))
+                start += width
 
         bias_rows = keep.tile([P, UNITS], BF16)
         nc.vector.memset(bias_rows[:].bitcast(I32), 0)
 
-        load_chunk(0, pieces=2)
+        load_unit(0, pieces=FIRST_PIECES)
+        load_unit(1)
         load_row_set(1)
-        load_chunk(1)
         for gate in range(GATES):
             nc.sync.dma_start(out=bias_rows[gate : gate + 1, :], in_=biases[gate].unsqueeze(0))
-        load_row_set(2)
-        load_chunk(2)
-        load_row_set(3)
-        load_chunk(3)
-        load_row_set(4)
-        for c in range(4, PREFETCH):
-            load_chunk(c)
+        for c in range(2, PREFETCH):
+            load_unit(c)
+            if c % 2 == 1 and 1 + c // 2 < len(row_sets):
+                load_row_set(1 + c // 2)
 
         pick = keep.tile([P, LAST], BF16)
         nc.vector.tensor_tensor(
@@ -156,60 +170,72 @@ def tile_multidimensinalgrucell_pb_kernel(
         codes_of = {}
         sums = {}
 
-        def regroup(c, pieces=1):
-            b, g = CHUNKS[c]
-            gate, first, width, share = BLOCKS[b]
-            raw = raw_of[c]
-            grouped = grouped_pool.tile([P, width, PACK], BF16, align_bytes=64, name="grouped")
-            piece = width // pieces
-            mine = int(piece * share) // 8 * 8
-            for i in range(pieces):
-                lo, mid, hi = i * piece, i * piece + mine, (i + 1) * piece
-                nc.vector.tensor_copy(
-                    out=grouped[:, lo:mid, :].rearrange("p (c i) t -> p c t i", i=4),
-                    in_=raw[:, :, lo:mid].rearrange("p t (c i) -> p c t i", i=4),
-                )
-                nc.scalar.copy(
-                    out=grouped[:, mid:hi, :].rearrange("p (c i) t -> p c t i", i=4),
-                    in_=raw[:, :, mid:hi].rearrange("p t (c i) -> p c t i", i=4),
-                )
-            grouped_of[c] = grouped
+        def pieces_of(c):
+            share = BLOCKS[units[c][0]][3]
+            shares = []
+            for start, width, part in raw_of[c]:
+                pieces = FIRST_PIECES if c == 0 else 1
+                piece = width // pieces
+                mine = int(piece * share) // 8 * 8
+                for i in range(pieces):
+                    shares.append((start, part, i * piece, i * piece + mine, (i + 1) * piece))
+            return shares
+
+        def regroup(copy, c, start, part, lo, hi):
+            copy(
+                out=grouped_of[c][:, start + lo : start + hi, :].rearrange("p (c i) t -> p c t i", i=4),
+                in_=part[:, :, lo:hi].rearrange("p t (c i) -> p c t i", i=4),
+            )
+
+        def regroup_scalar(c):
+            grouped_of[c] = grouped_pool.tile([P, UNITS, PACK], BF16, align_bytes=64, name="grouped")
+            for start, part, lo, mid, hi in pieces_of(c):
+                regroup(nc.scalar.copy, c, start, part, mid, hi)
+
+        def regroup_vector(c):
+            for start, part, lo, mid, hi in pieces_of(c):
+                regroup(nc.vector.tensor_copy, c, start, part, lo, mid)
 
         def quantise(c):
-            b, g = CHUNKS[c]
-            width = BLOCKS[b][2]
-            w_codes = code_pool.tile([P, width], U32, align_bytes=64, name="w_codes")
-            w_scales = code_pool.tile([P, width], U8, align_bytes=64, name="w_scales")
-            nc.vector.quantize_mx(
-                out=w_codes[:].bitcast(FP8X4),
-                scales=w_scales[:],
-                in_=grouped_of[c][:].rearrange("p w t -> p (w t)"),
-            )
+            w_codes = code_pool.tile([P, UNITS], U32, align_bytes=64, name="w_codes")
+            w_scales = code_pool.tile([P, UNITS], U8, align_bytes=64, name="w_scales")
+            pieces = LAST_PIECES if c == len(units) - 1 else 1
+            piece = UNITS // pieces
+            for i in range(pieces):
+                cols = slice(i * piece, (i + 1) * piece)
+                nc.vector.quantize_mx(
+                    out=w_codes[:, cols].bitcast(FP8X4),
+                    scales=w_scales[:, cols],
+                    in_=grouped_of[c][:, cols, :].rearrange("p w t -> p (w t)"),
+                )
             codes_of[c] = (w_codes, w_scales)
 
         next_bank = [0]
 
         def multiply(c):
-            b, g = CHUNKS[c]
-            gate, first, width, share = BLOCKS[b]
+            b, parts = units[c]
+            gate = BLOCKS[b][0]
             w_codes, w_scales = codes_of[c]
-            for m in range(BATCH_TILES):
-                rows = slice(m * P, (m + 1) * P)
-                for i in range(width // HALF):
-                    h = first // HALF + i
-                    cols = slice(i * HALF, (i + 1) * HALF)
-                    if g == 0:
-                        sums[(gate, h, m)] = bank([P, HALF], F32, next_bank[0] % BANKS)
-                        next_bank[0] += 1
-                    nc.tensor.matmul_mx(
-                        out=sums[(gate, h, m)][:],
-                        lhsT=q_codes[:, g, rows].bitcast(FP8X4),
-                        lhsT_scale=q_scales[:, g, rows],
-                        rhs=w_codes[:, cols].bitcast(FP8X4),
-                        rhs_scale=w_scales[:, cols],
-                        start=(g == 0),
-                        stop=(g == PASSES - 1),
-                    )
+            start = 0
+            for g, first, width in parts:
+                for m in range(BATCH_TILES):
+                    rows = slice(m * P, (m + 1) * P)
+                    for i in range(width // HALF):
+                        h = first // HALF + i
+                        cols = slice(start + i * HALF, start + (i + 1) * HALF)
+                        if g == 0:
+                            sums[(gate, h, m)] = bank([P, HALF], F32, next_bank[0] % BANKS)
+                            next_bank[0] += 1
+                        nc.tensor.matmul_mx(
+                            out=sums[(gate, h, m)][:],
+                            lhsT=q_codes[:, g, rows].bitcast(FP8X4),
+                            lhsT_scale=q_scales[:, g, rows],
+                            rhs=w_codes[:, cols].bitcast(FP8X4),
+                            rhs_scale=w_scales[:, cols],
+                            start=(g == 0),
+                            stop=(g == PASSES - 1),
+                        )
+                start += width
 
         tensor_tensor = nc.vector.tensor_tensor
         shape = [P, BATCH_TILES, HALF]
@@ -263,35 +289,50 @@ def tile_multidimensinalgrucell_pb_kernel(
 
         weighted = {}
 
-        def add_two(h):
-            total[h] = scratch.tile(shape, F32, name="total%d" % h)
-            tensor_tensor(out=total[h][:], in0=logits[h][:, 0, :, :], in1=logits[h][:, 1, :, :], op=ALU.add)
+        def add_up(first, terms):
+            added = {}
+            for m in range(BATCH_TILES):
+                added[m] = bank([P, HALF], F32, first + m)
+                for gate in range(LAST):
+                    nc.tensor.matmul(
+                        out=added[m][:],
+                        lhsT=ident_f32[:],
+                        rhs=terms[:, gate, m, :],
+                        start=(gate == 0),
+                        stop=(gate == LAST - 1),
+                    )
+            return added
 
-        def add_three(h):
-            tensor_tensor(out=total[h][:], in0=total[h][:], in1=logits[h][:, 2, :, :], op=ALU.add)
+        def add_weights(h):
+            totals[h] = add_up(6 * h, logits[h])
 
-        def logarithm(h):
-            gap[h] = scratch.tile(shape, F32, name="log_total%d" % h)
-            nc.scalar.activation(out=gap[h][:], in_=total[h][:], func=ACT.Ln)
-
-        def one_over_total(h):
-            nc.scalar.activation(out=total[h][:], in_=gap[h][:], func=ACT.Exp, scale=-1.0)
-
-        def blend_two(h):
+        def add_products(h):
+            blends[h] = add_up(2 - 2 * h, weighted[h])
             mean[h] = weighted[h][:, 0, :, :]
             lean[h] = weighted[h][:, 1, :, :]
-            tensor_tensor(out=mean[h], in0=mean[h], in1=lean[h], op=ALU.add)
 
-        def blend_three(h):
-            tensor_tensor(out=mean[h], in0=mean[h], in1=weighted[h][:, 2, :, :], op=ALU.add)
+        totals = {}
+        blends = {}
+
+        def logarithm(h):
+            gap[h] = logits[h][:, 1, :, :]
+            for m in range(BATCH_TILES):
+                nc.scalar.activation(out=gap[h][:, m, :], in_=totals[h][m][:], func=ACT.Ln)
+
+        def one_over_total(h):
+            total[h] = logits[h][:, 0, :, :]
+            nc.scalar.activation(out=total[h], in_=gap[h], func=ACT.Exp, scale=-1.0)
 
         def minus_lse(h):
             nc.vector.scalar_tensor_tensor(
-                out=gap[h][:], in0=peak[h][:], scalar=-1.0, in1=gap[h][:], op0=ALU.mult, op1=ALU.subtract
+                out=gap[h], in0=peak[h][:], scalar=-1.0, in1=gap[h], op0=ALU.mult, op1=ALU.subtract
             )
 
         def divide(h):
-            tensor_tensor(out=mean[h], in0=mean[h], in1=total[h][:], op=ALU.mult)
+            for m in range(BATCH_TILES):
+                tensor_tensor(
+                    out=mean[h][:, m, :], in0=blends[h][m][:], in1=total[h][:, m, :], op=ALU.mult
+                )
 
         def distance(h):
             cols = slice(h * HALF, (h + 1) * HALF)
@@ -323,51 +364,53 @@ def tile_multidimensinalgrucell_pb_kernel(
         def at(turn, fn, *args):
             plan.setdefault(turn, []).append((fn, args))
 
-        end = {b: (b + 1) * PASSES + 2 for b in range(len(BLOCKS))}
+        end = {}
+        for c, (b, parts) in enumerate(units):
+            end[b] = c + 3
         for h in range(HALVES):
-            at(end[0] + h, add_bias, 0, h)
+            at(end[0] + 1 + h, add_bias, 0, h)
             at(end[1] + h, add_bias, 1, h)
             at(end[1] + 2 + h, peak_two, h)
-            at(end[2], add_bias, 2, h)
+        t = end[2]
         for h in range(HALVES):
-            t = end[2] + 1 + h
+            at(t, add_bias, 2, h)
             at(t, peak_three, h)
-            at(t + 1, subtract_peak, h)
+            at(t + h, subtract_peak, h)
             at(t + 1, exponentials, h)
-            at(t + 2, add_two, h)
-            at(t + 2, weigh, h)
-            at(t + 3, add_three, h)
+            at(t + 1 + h, add_weights, h)
+            at(t + 2 + h, weigh, h)
+        for fn in (logarithm, one_over_total, add_products, minus_lse):
+            for h in range(HALVES):
+                at(t + (4 if fn == minus_lse else 3), fn, h)
         for h in range(HALVES):
-            at(end[2] + 5, logarithm, h)
-        for h in range(HALVES):
-            at(end[2] + 5, one_over_total, h)
-        for h in range(HALVES):
-            at(end[2] + 5, blend_two, h)
-            at(end[2] + 6, blend_three, h)
-            at(end[2] + 6, minus_lse, h)
-            at(end[2] + 7, divide, h)
-            at(end[2] + 8 + h, distance, h)
-            t = end[3 + h]
-            at(t + 1 - h, last_gate, h)
-            at(t + 2 - h, join_and_store, h)
+            at(t + 4 + 2 * h, divide, h)
+            at(t + 5 + 2 * h, distance, h)
+            at(end[3 + h] + h, last_gate, h)
+            at(end[3 + h] + 1, join_and_store, h)
 
-        count = len(CHUNKS)
+        count = len(units)
+        multiplied = 0
         for c in range(max(max(plan) + 1, count + 2)):
-            if c + PREFETCH < count:
-                load_chunk(c + PREFETCH)
+            ahead = c + PREFETCH
+            if ahead < count:
+                load_unit(ahead)
+                if ahead % 2 == 1 and 1 + ahead // 2 < len(row_sets):
+                    load_row_set(1 + ahead // 2)
             if c == PASSES:
                 load_row_set(0)
+            if Q_LAG <= c < PASSES + Q_LAG:
+                turn_q(c - Q_LAG)
             if c < count:
-                regroup(c, pieces=2 if c == 0 else 1)
-            if c < PASSES:
-                turn_q(c)
+                regroup_scalar(c)
+                regroup_vector(c)
             if 2 <= c < 2 + LAST:
                 spread_bias(c - 2)
             if 1 <= c <= count:
                 quantise(c - 1)
-            if 1 <= c <= PASSES:
-                quantise_q(c - 1)
-            if 2 <= c < count + 2:
-                multiply(c - 2)
+            if Q_LAG <= c < PASSES + Q_LAG:
+                quantise_q(c - Q_LAG)
+            while multiplied < min(count, c - 1) and (multiplied >= PASSES or multiplied < c - Q_LAG):
+                multiply(multiplied)
+                multiplied += 1
             for fn, args in plan.get(c, []):
                 fn(*args)

@@ -35,6 +35,7 @@ BLOCKS = [
     (3, 0, HALF, 0.42),
     (3, HALF, HALF, 0.28),
 ]
+RUN = 2
 PREFETCH = 5
 LAST_PIECES = 2
 FIRST_PIECES = 2
@@ -183,8 +184,8 @@ def tile_multidimensinalgrucell_pb_kernel(
 
         def regroup(copy, c, start, part, lo, hi):
             copy(
-                out=grouped_of[c][:, start + lo : start + hi, :].rearrange("p (c i) t -> p c t i", i=4),
-                in_=part[:, :, lo:hi].rearrange("p t (c i) -> p c t i", i=4),
+                out=grouped_of[c][:, start + lo : start + hi, :].rearrange("p (c i) t -> p c t i", i=RUN),
+                in_=part[:, :, lo:hi].rearrange("p t (c i) -> p c t i", i=RUN),
             )
 
         def regroup_scalar(c):

@@ -29,12 +29,14 @@ BANKS = 8
 FLOPS = 2 * BATCH * K_ALL * GATES * UNITS
 
 BLOCKS = [
-    (0, 0, UNITS, 0.60),
-    (1, 0, UNITS, 0.52),
-    (2, 0, UNITS, 0.42),
-    (3, 0, HALF, 0.42),
-    (3, HALF, HALF, 0.28),
+    (0, 0, UNITS, (0.62, 0.62)),
+    (1, 0, UNITS, (0.52, 0.52)),
+    (2, 0, HALF, (0.36, 0.36)),
+    (2, HALF, HALF, (0.34, 0.34)),
+    (3, 0, HALF, (0.36, 0.36)),
+    (3, HALF, HALF, (0.60, 0.25)),
 ]
+FIRST_BANK = [0, 4, 0, 2, 4, 2]
 RUN = 2
 PREFETCH = 5
 LAST_PIECES = 2
@@ -172,7 +174,10 @@ def tile_multidimensinalgrucell_pb_kernel(
         sums = {}
 
         def pieces_of(c):
-            share = BLOCKS[units[c][0]][3]
+            b = units[c][0]
+            members = [i for i in range(len(units)) if units[i][0] == b]
+            low, high = BLOCKS[b][3]
+            share = low + (high - low) * members.index(c) / (len(members) - 1)
             shares = []
             for start, width, part in raw_of[c]:
                 pieces = FIRST_PIECES if c == 0 else 1
@@ -211,8 +216,6 @@ def tile_multidimensinalgrucell_pb_kernel(
                 )
             codes_of[c] = (w_codes, w_scales)
 
-        next_bank = [0]
-
         def multiply(c):
             b, parts = units[c]
             gate = BLOCKS[b][0]
@@ -225,8 +228,8 @@ def tile_multidimensinalgrucell_pb_kernel(
                         h = first // HALF + i
                         cols = slice(start + i * HALF, start + (i + 1) * HALF)
                         if g == 0:
-                            sums[(gate, h, m)] = bank([P, HALF], F32, next_bank[0] % BANKS)
-                            next_bank[0] += 1
+                            index = FIRST_BANK[b] + m * (width // HALF) + i
+                            sums[(gate, h, m)] = bank([P, HALF], F32, index)
                         nc.tensor.matmul_mx(
                             out=sums[(gate, h, m)][:],
                             lhsT=q_codes[:, g, rows].bitcast(FP8X4),
@@ -305,10 +308,10 @@ def tile_multidimensinalgrucell_pb_kernel(
             return added
 
         def add_weights(h):
-            totals[h] = add_up(6 * h, logits[h])
+            totals[h] = add_up(2 * h, logits[h])
 
         def add_products(h):
-            blends[h] = add_up(2 - 2 * h, weighted[h])
+            blends[h] = add_up(6 - 6 * h, weighted[h])
             mean[h] = weighted[h][:, 0, :, :]
             lean[h] = weighted[h][:, 1, :, :]
 
@@ -372,22 +375,28 @@ def tile_multidimensinalgrucell_pb_kernel(
             at(end[0] + 1 + h, add_bias, 0, h)
             at(end[1] + h, add_bias, 1, h)
             at(end[1] + 2 + h, peak_two, h)
-        t = end[2]
         for h in range(HALVES):
+            t = end[2 + h]
             at(t, add_bias, 2, h)
             at(t, peak_three, h)
-            at(t + h, subtract_peak, h)
+            at(t, subtract_peak, h)
             at(t + 1, exponentials, h)
-            at(t + 1 + h, add_weights, h)
-            at(t + 2 + h, weigh, h)
-        for fn in (logarithm, one_over_total, add_products, minus_lse):
+            at(t + 1, add_weights, h)
+            at(t + 2, weigh, h)
+        at(end[2] + 3, add_products, 0)
+        t = end[3] + 3
+        for fn in (logarithm, one_over_total):
             for h in range(HALVES):
-                at(t + (4 if fn == minus_lse else 3), fn, h)
+                at(t, fn, h)
+        at(t, add_products, 1)
         for h in range(HALVES):
-            at(t + 4 + 2 * h, divide, h)
-            at(t + 5 + 2 * h, distance, h)
-            at(end[3 + h] + h, last_gate, h)
-            at(end[3 + h] + 1, join_and_store, h)
+            at(t + 1, minus_lse, h)
+            at(t + 1 + h, divide, h)
+            at(t + 2 + h, distance, h)
+        at(end[4] + 1, last_gate, 0)
+        at(end[4] + 2, join_and_store, 0)
+        at(end[5], last_gate, 1)
+        at(end[5] + 1, join_and_store, 1)
 
         count = len(units)
         multiplied = 0

@@ -31,17 +31,17 @@ FLOPS = 2 * BATCH * K_ALL * GATES * UNITS
 BLOCKS = [
     (0, 0, UNITS, (0.62, 0.62)),
     (1, 0, UNITS, (0.52, 0.52)),
-    (2, 0, HALF, (0.36, 0.36)),
-    (2, HALF, HALF, (0.34, 0.34)),
-    (3, 0, HALF, (0.36, 0.36)),
-    (3, HALF, HALF, (0.60, 0.25)),
+    (2, 0, HALF, (0.35, 0.35)),
+    (2, HALF, HALF, (0.35, 0.35)),
+    (3, 0, HALF, (0.35, 0.35)),
+    (3, HALF, HALF, (0.60, 0.20)),
 ]
 FIRST_BANK = [0, 4, 0, 2, 4, 2]
 RUN = 2
 PREFETCH = 5
 LAST_PIECES = 2
 FIRST_PIECES = 2
-Q_LAG = 2
+Q_LAG = 4
 
 
 def units_of(blocks):
@@ -69,7 +69,7 @@ def tile_multidimensinalgrucell_pb_kernel(
         q_stage = stack.enter_context(tc.tile_pool(name="q_stage", bufs=2))
         raw_pool = stack.enter_context(tc.tile_pool(name="raw", bufs=PREFETCH + 2))
         grouped_pool = stack.enter_context(tc.tile_pool(name="grouped", bufs=4))
-        code_pool = stack.enter_context(tc.tile_pool(name="codes", bufs=4))
+        code_pool = stack.enter_context(tc.tile_pool(name="codes", bufs=6))
         scratch = stack.enter_context(tc.tile_pool(name="scratch", bufs=1))
         psum = stack.enter_context(tc.psum_pool(name="psum", bufs=1))
 
@@ -111,15 +111,17 @@ def tile_multidimensinalgrucell_pb_kernel(
         bias_rows = keep.tile([P, UNITS], BF16)
         nc.vector.memset(bias_rows[:].bitcast(I32), 0)
 
-        load_unit(0, pieces=FIRST_PIECES)
-        load_unit(1)
-        load_row_set(1)
-        for gate in range(GATES):
-            nc.sync.dma_start(out=bias_rows[gate : gate + 1, :], in_=biases[gate].unsqueeze(0))
-        for c in range(2, PREFETCH):
-            load_unit(c)
-            if c % 2 == 1 and 1 + c // 2 < len(row_sets):
-                load_row_set(1 + c // 2)
+        def load_ahead(c):
+            load_unit(c, pieces=FIRST_PIECES if c == 0 else 1)
+            if c == 1:
+                for gate in range(GATES):
+                    nc.sync.dma_start(out=bias_rows[gate : gate + 1, :], in_=biases[gate].unsqueeze(0))
+            s, odd = divmod(c - (Q_LAG - 1), 2)
+            if odd == 0 and 0 <= s < len(row_sets) - 1:
+                load_row_set(1 + s)
+
+        for c in range(PREFETCH):
+            load_ahead(c)
 
         pick = keep.tile([P, LAST], BF16)
         nc.vector.tensor_tensor(
@@ -372,7 +374,7 @@ def tile_multidimensinalgrucell_pb_kernel(
         for c, (b, parts) in enumerate(units):
             end[b] = c + 3
         for h in range(HALVES):
-            at(end[0] + 1 + h, add_bias, 0, h)
+            at(end[0] + Q_LAG - 1 + h, add_bias, 0, h)
             at(end[1] + h, add_bias, 1, h)
             at(end[1] + 2 + h, peak_two, h)
         for h in range(HALVES):
@@ -392,21 +394,19 @@ def tile_multidimensinalgrucell_pb_kernel(
         for h in range(HALVES):
             at(t + 1, minus_lse, h)
             at(t + 1 + h, divide, h)
-            at(t + 2 + h, distance, h)
-        at(end[4] + 1, last_gate, 0)
+            at(t + 2, distance, h)
+        at(end[4], last_gate, 0)
         at(end[4] + 2, join_and_store, 0)
         at(end[5], last_gate, 1)
-        at(end[5] + 1, join_and_store, 1)
+        at(end[5], join_and_store, 1)
 
         count = len(units)
         multiplied = 0
         for c in range(max(max(plan) + 1, count + 2)):
             ahead = c + PREFETCH
             if ahead < count:
-                load_unit(ahead)
-                if ahead % 2 == 1 and 1 + ahead // 2 < len(row_sets):
-                    load_row_set(1 + ahead // 2)
-            if c == PASSES:
+                load_ahead(ahead)
+            if c == 2 * PASSES:
                 load_row_set(0)
             if Q_LAG <= c < PASSES + Q_LAG:
                 turn_q(c - Q_LAG)

@@ -31,10 +31,10 @@ FLOPS = 2 * BATCH * K_ALL * GATES * UNITS
 BLOCKS = [
     (0, 0, UNITS, (0.62, 0.62)),
     (1, 0, UNITS, (0.52, 0.52)),
-    (2, 0, HALF, (0.35, 0.35)),
-    (2, HALF, HALF, (0.35, 0.35)),
-    (3, 0, HALF, (0.35, 0.35)),
-    (3, HALF, HALF, (0.60, 0.20)),
+    (2, 0, HALF, (0.34, 0.34)),
+    (2, HALF, HALF, (0.34, 0.34)),
+    (3, 0, HALF, (0.34, 0.34)),
+    (3, HALF, HALF, (0.60, 0.40)),
 ]
 FIRST_BANK = [0, 4, 0, 2, 4, 2]
 RUN = 2
@@ -295,54 +295,86 @@ def tile_multidimensinalgrucell_pb_kernel(
 
         weighted = {}
 
+        turned_shape = [P, HALF // P, P]
+
         def add_up(first, terms):
             added = {}
             for m in range(BATCH_TILES):
-                added[m] = bank([P, HALF], F32, first + m)
-                for gate in range(LAST):
-                    nc.tensor.matmul(
-                        out=added[m][:],
-                        lhsT=ident_f32[:],
-                        rhs=terms[:, gate, m, :],
-                        start=(gate == 0),
-                        stop=(gate == LAST - 1),
-                    )
+                added[m] = bank(turned_shape, F32, first + m)
+                for j in range(HALF // P):
+                    for gate in range(LAST):
+                        nc.tensor.matmul(
+                            out=added[m][:, j, :],
+                            lhsT=terms[:, gate, m, j * P : (j + 1) * P],
+                            rhs=ident_f32[:],
+                            start=(gate == 0),
+                            stop=(gate == LAST - 1),
+                            is_transpose=True,
+                        )
             return added
 
+        def turn_back(first, turned, cols=None):
+            back = {}
+            for m in range(BATCH_TILES):
+                back[m] = bank([P, HALF], F32, first + m)
+                for j in range(HALF // P):
+                    block = slice(j * P, (j + 1) * P)
+                    if cols is not None:
+                        nc.tensor.matmul(
+                            out=back[m][:, block],
+                            lhsT=ident_bf16[:],
+                            rhs=rows_in[:, LAST, m, cols][:, block],
+                            start=True,
+                            stop=False,
+                        )
+                    nc.tensor.matmul(
+                        out=back[m][:, block],
+                        lhsT=turned[:, m, block],
+                        rhs=ident_f32[:],
+                        start=(cols is None),
+                        stop=True,
+                        is_transpose=True,
+                    )
+            return back
+
+        totals = {}
+        blends = {}
+        log_back = {}
+
         def add_weights(h):
-            totals[h] = add_up(2 * h, logits[h])
+            totals[h] = add_up(BATCH_TILES * h, logits[h])
 
         def add_products(h):
             blends[h] = add_up(6 - 6 * h, weighted[h])
             mean[h] = weighted[h][:, 0, :, :]
-            lean[h] = weighted[h][:, 1, :, :]
-
-        totals = {}
-        blends = {}
 
         def logarithm(h):
             gap[h] = logits[h][:, 1, :, :]
             for m in range(BATCH_TILES):
-                nc.scalar.activation(out=gap[h][:, m, :], in_=totals[h][m][:], func=ACT.Ln)
+                nc.scalar.activation(
+                    out=gap[h][:, m, :], in_=totals[h][m][:].rearrange("p j b -> p (j b)"), func=ACT.Ln
+                )
+            log_back[h] = turn_back(BATCH_TILES * h, gap[h])
 
         def one_over_total(h):
             total[h] = logits[h][:, 0, :, :]
             nc.scalar.activation(out=total[h], in_=gap[h], func=ACT.Exp, scale=-1.0)
 
         def minus_lse(h):
-            nc.vector.scalar_tensor_tensor(
-                out=gap[h], in0=peak[h][:], scalar=-1.0, in1=gap[h], op0=ALU.mult, op1=ALU.subtract
-            )
+            gap[h] = logits[h][:, 2, :, :]
+            for m in range(BATCH_TILES):
+                nc.vector.scalar_tensor_tensor(
+                    out=gap[h][:, m, :], in0=peak[h][:, m, :], scalar=-1.0, in1=log_back[h][m][:],
+                    op0=ALU.mult, op1=ALU.subtract,
+                )
 
         def divide(h):
             for m in range(BATCH_TILES):
-                tensor_tensor(
-                    out=mean[h][:, m, :], in0=blends[h][m][:], in1=total[h][:, m, :], op=ALU.mult
+                nc.vector.scalar_tensor_tensor(
+                    out=mean[h][:, m, :], in0=blends[h][m][:].rearrange("p j b -> p (j b)"), scalar=-1.0,
+                    in1=total[h][:, m, :], op0=ALU.mult, op1=ALU.mult,
                 )
-
-        def distance(h):
-            cols = slice(h * HALF, (h + 1) * HALF)
-            tensor_tensor(out=lean[h], in0=rows_in[:, LAST, :, cols], in1=mean[h], op=ALU.subtract)
+            lean[h] = turn_back(6 - 6 * h, mean[h], slice(h * HALF, (h + 1) * HALF))
 
         def last_gate(h):
             for m in range(BATCH_TILES):
@@ -355,12 +387,12 @@ def tile_multidimensinalgrucell_pb_kernel(
             cols = slice(h * HALF, (h + 1) * HALF)
             for m in range(BATCH_TILES):
                 nc.vector.scalar_tensor_tensor(
-                    out=lean[h][:, m, :], in0=gap[h][:, m, :], scalar=1.0, in1=lean[h][:, m, :],
+                    out=gap[h][:, m, :], in0=gap[h][:, m, :], scalar=-1.0, in1=lean[h][m][:],
                     op0=ALU.add, op1=ALU.mult,
                 )
             for m in range(BATCH_TILES):
                 nc.vector.scalar_tensor_tensor(
-                    out=mean[h][:, m, :], in0=lean[h][:, m, :], scalar=0.5, in1=mean[h][:, m, :],
+                    out=mean[h][:, m, :], in0=gap[h][:, m, :], scalar=0.5, in1=rows_in[:, LAST, m, cols],
                     op0=ALU.mult, op1=ALU.add,
                 )
                 nc.sync.dma_start(out=out[m * P : (m + 1) * P, cols], in_=mean[h][:, m, :])
@@ -381,21 +413,19 @@ def tile_multidimensinalgrucell_pb_kernel(
             t = end[2 + h]
             at(t, add_bias, 2, h)
             at(t, peak_three, h)
-            at(t, subtract_peak, h)
-            at(t + 1, exponentials, h)
-            at(t + 1, add_weights, h)
+            at(t + h, subtract_peak, h)
+            at(t + 1 + h, exponentials, h)
+            at(t + 1 + h, add_weights, h)
             at(t + 2, weigh, h)
         at(end[2] + 3, add_products, 0)
-        t = end[3] + 3
-        for fn in (logarithm, one_over_total):
+        t = end[3] + 2
+        for fn in (logarithm, one_over_total, minus_lse):
             for h in range(HALVES):
                 at(t, fn, h)
         at(t, add_products, 1)
         for h in range(HALVES):
-            at(t + 1, minus_lse, h)
-            at(t + 1 + h, divide, h)
-            at(t + 2, distance, h)
-        at(end[4], last_gate, 0)
+            at(t, divide, h)
+        at(end[4] + 1, last_gate, 0)
         at(end[4] + 2, join_and_store, 0)
         at(end[5], last_gate, 1)
         at(end[5], join_and_store, 1)

@@ -37,7 +37,8 @@ BLOCKS = [
     (3, HALF, HALF, (0.60, 0.40)),
 ]
 FIRST_BANK = [0, 4, 0, 2, 4, 2]
-RUN = 2
+SCALAR_RUN = 2
+VECTOR_RUN = 4
 PREFETCH = 5
 LAST_PIECES = 2
 FIRST_PIECES = 2
@@ -189,20 +190,20 @@ def tile_multidimensinalgrucell_pb_kernel(
                     shares.append((start, part, i * piece, i * piece + mine, (i + 1) * piece))
             return shares
 
-        def regroup(copy, c, start, part, lo, hi):
+        def regroup(copy, run, c, start, part, lo, hi):
             copy(
-                out=grouped_of[c][:, start + lo : start + hi, :].rearrange("p (c i) t -> p c t i", i=RUN),
-                in_=part[:, :, lo:hi].rearrange("p t (c i) -> p c t i", i=RUN),
+                out=grouped_of[c][:, start + lo : start + hi, :].rearrange("p (c i) t -> p c t i", i=run),
+                in_=part[:, :, lo:hi].rearrange("p t (c i) -> p c t i", i=run),
             )
 
         def regroup_scalar(c):
             grouped_of[c] = grouped_pool.tile([P, UNITS, PACK], BF16, align_bytes=64, name="grouped")
             for start, part, lo, mid, hi in pieces_of(c):
-                regroup(nc.scalar.copy, c, start, part, mid, hi)
+                regroup(nc.scalar.copy, SCALAR_RUN, c, start, part, mid, hi)
 
         def regroup_vector(c):
             for start, part, lo, mid, hi in pieces_of(c):
-                regroup(nc.vector.tensor_copy, c, start, part, lo, mid)
+                regroup(nc.vector.tensor_copy, VECTOR_RUN, c, start, part, lo, mid)
 
         def quantise(c):
             w_codes = code_pool.tile([P, UNITS], U32, align_bytes=64, name="w_codes")

@@ -29,19 +29,18 @@ BANKS = 8
 FLOPS = 2 * BATCH * K_ALL * GATES * UNITS
 
 BLOCKS = [
-    (0, 0, UNITS, (0.62, 0.62)),
-    (1, 0, UNITS, (0.52, 0.52)),
-    (2, 0, HALF, (0.34, 0.34)),
-    (2, HALF, HALF, (0.34, 0.34)),
-    (3, 0, HALF, (0.34, 0.34)),
-    (3, HALF, HALF, (0.60, 0.40)),
+    (0, 0, UNITS, (0.55, 0.55)),
+    (1, 0, UNITS, (0.51, 0.51)),
+    (2, 0, HALF, (0.31, 0.31)),
+    (2, HALF, HALF, (0.31, 0.31)),
+    (3, 0, HALF, (0.28, 0.28)),
+    (3, HALF, HALF, (0.60, 0.35)),
 ]
 FIRST_BANK = [0, 4, 0, 2, 4, 2]
 SCALAR_RUN = 2
 VECTOR_RUN = 4
 PREFETCH = 5
 LAST_PIECES = 2
-FIRST_PIECES = 2
 Q_LAG = 4
 
 
@@ -91,7 +90,7 @@ def tile_multidimensinalgrucell_pb_kernel(
 
         raw_of = {}
 
-        def load_unit(c, pieces=1):
+        def load_unit(c):
             b, parts = units[c]
             gate = BLOCKS[b][0]
             raw = raw_pool.tile([P, PACK * UNITS], BF16, name="raw")
@@ -100,12 +99,7 @@ def tile_multidimensinalgrucell_pb_kernel(
             for g, first, width in parts:
                 part = raw[:, start * PACK : (start + width) * PACK].rearrange("p (t w) -> p t w", t=PACK)
                 rows = weights[gate][g * K_PASS : (g + 1) * K_PASS, :].rearrange("(p t) w -> p t w", t=PACK)
-                piece = width // pieces
-                for i in range(pieces):
-                    nc.sync.dma_start(
-                        out=part[:, :, i * piece : (i + 1) * piece],
-                        in_=rows[:, :, first + i * piece : first + (i + 1) * piece],
-                    )
+                nc.sync.dma_start(out=part, in_=rows[:, :, first : first + width])
                 raw_of[c].append((start, width, part))
                 start += width
 
@@ -113,8 +107,8 @@ def tile_multidimensinalgrucell_pb_kernel(
         nc.vector.memset(bias_rows[:].bitcast(I32), 0)
 
         def load_ahead(c):
-            load_unit(c, pieces=FIRST_PIECES if c == 0 else 1)
-            if c == 1:
+            load_unit(c)
+            if c == 0:
                 for gate in range(GATES):
                     nc.sync.dma_start(out=bias_rows[gate : gate + 1, :], in_=biases[gate].unsqueeze(0))
             s, odd = divmod(c - (Q_LAG - 1), 2)
@@ -183,11 +177,8 @@ def tile_multidimensinalgrucell_pb_kernel(
             share = low + (high - low) * members.index(c) / (len(members) - 1)
             shares = []
             for start, width, part in raw_of[c]:
-                pieces = FIRST_PIECES if c == 0 else 1
-                piece = width // pieces
-                mine = int(piece * share) // 8 * 8
-                for i in range(pieces):
-                    shares.append((start, part, i * piece, i * piece + mine, (i + 1) * piece))
+                mine = int(width * share) // 8 * 8
+                shares.append((start, part, 0, mine, width))
             return shares
 
         def regroup(copy, run, c, start, part, lo, hi):
@@ -318,22 +309,19 @@ def tile_multidimensinalgrucell_pb_kernel(
             back = {}
             for m in range(BATCH_TILES):
                 back[m] = bank([P, HALF], F32, first + m)
+                if cols is not None:
+                    nc.tensor.matmul(
+                        out=back[m][:], lhsT=ident_bf16[:], rhs=rows_in[:, LAST, m, cols], start=True, stop=False
+                    )
+            for m in range(BATCH_TILES):
                 for j in range(HALF // P):
                     block = slice(j * P, (j + 1) * P)
-                    if cols is not None:
-                        nc.tensor.matmul(
-                            out=back[m][:, block],
-                            lhsT=ident_bf16[:],
-                            rhs=rows_in[:, LAST, m, cols][:, block],
-                            start=True,
-                            stop=False,
-                        )
                     nc.tensor.matmul(
                         out=back[m][:, block],
                         lhsT=turned[:, m, block],
                         rhs=ident_f32[:],
                         start=(cols is None),
-                        stop=True,
+                        stop=(cols is None or block.stop == HALF),
                         is_transpose=True,
                     )
             return back
@@ -407,25 +395,25 @@ def tile_multidimensinalgrucell_pb_kernel(
         for c, (b, parts) in enumerate(units):
             end[b] = c + 3
         for h in range(HALVES):
-            at(end[0] + Q_LAG - 1 + h, add_bias, 0, h)
-            at(end[1] + h, add_bias, 1, h)
-            at(end[1] + 2 + h, peak_two, h)
+            at(end[0] + Q_LAG - 1, add_bias, 0, h)
+            at(end[1], add_bias, 1, h)
+            at(end[1] + 1 + h, peak_two, h)
         for h in range(HALVES):
             t = end[2 + h]
             at(t, add_bias, 2, h)
             at(t, peak_three, h)
             at(t + h, subtract_peak, h)
-            at(t + 1 + h, exponentials, h)
+            at(t + 1, exponentials, h)
             at(t + 1 + h, add_weights, h)
-            at(t + 2, weigh, h)
+            at(t + 1, weigh, h)
         at(end[2] + 3, add_products, 0)
         t = end[3] + 2
         for fn in (logarithm, one_over_total, minus_lse):
             for h in range(HALVES):
                 at(t, fn, h)
-        at(t, add_products, 1)
+        at(t + 1, add_products, 1)
         for h in range(HALVES):
-            at(t, divide, h)
+            at(t + 1, divide, h)
         at(end[4] + 1, last_gate, 0)
         at(end[4] + 2, join_and_store, 0)
         at(end[5], last_gate, 1)
@@ -441,11 +429,11 @@ def tile_multidimensinalgrucell_pb_kernel(
                 load_row_set(0)
             if Q_LAG <= c < PASSES + Q_LAG:
                 turn_q(c - Q_LAG)
+            if 1 <= c <= LAST:
+                spread_bias(c - 1)
             if c < count:
                 regroup_scalar(c)
                 regroup_vector(c)
-            if 2 <= c < 2 + LAST:
-                spread_bias(c - 2)
             if 1 <= c <= count:
                 quantise(c - 1)
             if Q_LAG <= c < PASSES + Q_LAG:

@@ -29,18 +29,23 @@ BANKS = 8
 FLOPS = 2 * BATCH * K_ALL * GATES * UNITS
 
 BLOCKS = [
-    (0, 0, UNITS, (0.55, 0.55)),
-    (1, 0, UNITS, (0.51, 0.51)),
-    (2, 0, HALF, (0.31, 0.31)),
-    (2, HALF, HALF, (0.31, 0.31)),
-    (3, 0, HALF, (0.28, 0.28)),
-    (3, HALF, HALF, (0.60, 0.35)),
+    (0, 0, UNITS, (0.52, 0.52)),
+    (1, 0, UNITS, (0.50, 0.50)),
+    (2, 0, HALF, (0.30, 0.30)),
+    (2, HALF, HALF, (0.30, 0.30)),
+    (3, 0, HALF, (0.26, 0.26)),
+    (3, HALF, HALF, (0.60, 0.25)),
 ]
 FIRST_BANK = [0, 4, 0, 2, 4, 2]
 SCALAR_RUN = 2
 VECTOR_RUN = 4
 PREFETCH = 5
 LAST_PIECES = 2
+MARKS = 5
+MARK_PITCH = 8
+LONG_STRETCH = 288
+SHORT_STRETCH = 96
+LSE_STRETCH = 192
 Q_LAG = 4
 
 
@@ -187,9 +192,34 @@ def tile_multidimensinalgrucell_pb_kernel(
                 in_=part[:, :, lo:hi].rearrange("p t (c i) -> p c t i", i=run),
             )
 
+        marks = keep.tile([P, MARKS, MARK_PITCH], F32)
+        gpsimd_cols = {}
+
+        def grouped_tile(c):
+            if c not in grouped_of:
+                grouped_of[c] = grouped_pool.tile([P, UNITS, PACK], BF16, align_bytes=64, name="grouped")
+            return grouped_of[c]
+
+        def regroup_gpsimd(i, jobs):
+            mark = marks[:, i, 0:1]
+            nc.vector.memset(mark, 1.0)
+            for c, cols in jobs:
+                gpsimd_cols[c] = cols
+                start, width, part = raw_of[c][-1]
+                nc.gpsimd.tensor_scalar(
+                    out=grouped_tile(c)[:, UNITS - cols : UNITS, :],
+                    in0=part[:, :, width - cols : width].rearrange("p t w -> p w t"),
+                    scalar1=mark,
+                    scalar2=0.0,
+                    op0=ALU.mult,
+                    op1=ALU.add,
+                )
+
         def regroup_scalar(c):
-            grouped_of[c] = grouped_pool.tile([P, UNITS, PACK], BF16, align_bytes=64, name="grouped")
+            grouped_tile(c)
             for start, part, lo, mid, hi in pieces_of(c):
+                if start + hi == UNITS:
+                    hi -= gpsimd_cols.get(c, 0)
                 regroup(nc.scalar.copy, SCALAR_RUN, c, start, part, mid, hi)
 
         def regroup_vector(c):
@@ -394,12 +424,15 @@ def tile_multidimensinalgrucell_pb_kernel(
         end = {}
         for c, (b, parts) in enumerate(units):
             end[b] = c + 3
+        at(end[0] + Q_LAG - 1, regroup_gpsimd, 0, [(end[0] + Q_LAG, LONG_STRETCH)])
+        at(end[1], regroup_gpsimd, 1, [(end[1] + 1, LONG_STRETCH)])
         for h in range(HALVES):
             at(end[0] + Q_LAG - 1, add_bias, 0, h)
             at(end[1], add_bias, 1, h)
             at(end[1] + 1 + h, peak_two, h)
         for h in range(HALVES):
             t = end[2 + h]
+            at(t, regroup_gpsimd, 2 + h, [(t + 1, SHORT_STRETCH)])
             at(t, add_bias, 2, h)
             at(t, peak_three, h)
             at(t + h, subtract_peak, h)
@@ -408,9 +441,12 @@ def tile_multidimensinalgrucell_pb_kernel(
             at(t + 1, weigh, h)
         at(end[2] + 3, add_products, 0)
         t = end[3] + 2
-        for fn in (logarithm, one_over_total, minus_lse):
+        for fn in (logarithm, one_over_total):
             for h in range(HALVES):
                 at(t, fn, h)
+        at(t + 1, regroup_gpsimd, 4, [(t + 2, LSE_STRETCH), (t + 3, LSE_STRETCH)])
+        for h in range(HALVES):
+            at(t + 1, minus_lse, h)
         at(t + 1, add_products, 1)
         for h in range(HALVES):
             at(t + 1, divide, h)

from contextlib import ExitStack

import concourse.mybir as mybir
from concourse.masks import make_identity

F32 = mybir.dt.float32
BF16 = mybir.dt.bfloat16
I32 = mybir.dt.int32
U32 = mybir.dt.uint32
U8 = mybir.dt.uint8
FP8X4 = mybir.dt.float8_e4m3fn_x4
ACT = mybir.ActivationFunctionType
ALU = mybir.AluOpType

P = 128
PACK = 4
K_PASS = P * PACK
BATCH = 256
UNITS = 1024
K_ALL = 4 * UNITS
GATES = 4
LAST = GATES - 1
BATCH_TILES = BATCH // P
PASSES = K_ALL // K_PASS
HALF = 512
HALVES = UNITS // HALF
BANKS = 8

FLOPS = 2 * BATCH * K_ALL * GATES * UNITS

BLOCKS = [
    (0, 0, UNITS, (0.52, 0.52)),
    (1, 0, UNITS, (0.50, 0.50)),
    (2, 0, HALF, (0.30, 0.30)),
    (2, HALF, HALF, (0.30, 0.30)),
    (3, 0, HALF, (0.26, 0.26)),
    (3, HALF, HALF, (0.60, 0.25)),
]
FIRST_BANK = [0, 4, 0, 2, 4, 2]
SCALAR_RUN = 2
VECTOR_RUN = 4
PREFETCH = 5
LAST_PIECES = 2
MARKS = 5
MARK_PITCH = 8
LONG_STRETCH = 288
SHORT_STRETCH = 96
LSE_STRETCH = 192
Q_LAG = 4


def units_of(blocks):
    units = []
    for b, (gate, first, width, share) in enumerate(blocks):
        span = UNITS // width
        for g in range(0, PASSES, span):
            units.append((b, [(g + i, first, width) for i in range(span)]))
    return units


def tile_multidimensinalgrucell_pb_kernel(
    tc, x, left_state, top_state, diagonal_state, h_cand,
    w_zi, b_zi, w_zl, b_zl, w_zt, b_zt, w_zd, b_zd, out,
):
    nc = tc.nc
    weights = [w_zi, w_zl, w_zt, w_zd]
    biases = [b_zi, b_zl, b_zt, b_zd]
    row_sets = [h_cand, left_state, top_state, diagonal_state, x]
    units = units_of(BLOCKS)

    with ExitStack() as stack:
        stack.enter_context(tc.manual_schedule())
        keep = stack.enter_context(tc.tile_pool(name="keep", bufs=1))
        q_stage = stack.enter_context(tc.tile_pool(name="q_stage", bufs=2))
        raw_pool = stack.enter_context(tc.tile_pool(name="raw", bufs=PREFETCH + 2))
        grouped_pool = stack.enter_context(tc.tile_pool(name="grouped", bufs=4))
        code_pool = stack.enter_context(tc.tile_pool(name="codes", bufs=6))
        scratch = stack.enter_context(tc.tile_pool(name="scratch", bufs=1))
        psum = stack.enter_context(tc.psum_pool(name="psum", bufs=1))

        def bank(shape, dtype, index):
            return psum.tile(shape, dtype, tag="bank%d" % index, name="bank%d" % index)

        ident_f32 = keep.tile([P, P], F32)
        make_identity(nc, ident_f32[:])
        ident_bf16 = keep.tile([P, P], BF16)
        make_identity(nc, ident_bf16[:])

        rows_in = keep.tile([P, len(row_sets), BATCH_TILES, UNITS], BF16)

        def load_row_set(s):
            nc.sync.dma_start(
                out=rows_in[:, s, :, :], in_=row_sets[s].rearrange("(m p) c -> p m c", p=P)
            )

        raw_of = {}

        def load_unit(c):
            b, parts = units[c]
            gate = BLOCKS[b][0]
            raw = raw_pool.tile([P, PACK * UNITS], BF16, name="raw")
            raw_of[c] = []
            start = 0
            for g, first, width in parts:
                part = raw[:, start * PACK : (start + width) * PACK].rearrange("p (t w) -> p t w", t=PACK)
                rows = weights[gate][g * K_PASS : (g + 1) * K_PASS, :].rearrange("(p t) w -> p t w", t=PACK)
                nc.sync.dma_start(out=part, in_=rows[:, :, first : first + width])
                raw_of[c].append((start, width, part))
                start += width

        bias_rows = keep.tile([P, UNITS], BF16)
        nc.vector.memset(bias_rows[:].bitcast(I32), 0)

        def load_ahead(c):
            load_unit(c)
            if c == 0:
                for gate in range(GATES):
                    nc.sync.dma_start(out=bias_rows[gate : gate + 1, :], in_=biases[gate].unsqueeze(0))
            s, odd = divmod(c - (Q_LAG - 1), 2)
            if odd == 0 and 0 <= s < len(row_sets) - 1:
                load_row_set(1 + s)

        for c in range(PREFETCH):
            load_ahead(c)

        pick = keep.tile([P, LAST], BF16)
        nc.vector.tensor_tensor(
            out=pick[:],
            in0=ident_bf16[:, 0:LAST],
            in1=ident_bf16[:, LAST : LAST + 1].to_broadcast([P, LAST]),
            op=ALU.subtract,
        )
        bias_gap = keep.tile([P, LAST, UNITS], F32)

        def spread_bias(gate):
            for h in range(HALVES):
                cols = slice(h * HALF, (h + 1) * HALF)
                spread = bank([P, HALF], F32, 4 + (gate * HALVES + h) % 4)
                nc.tensor.matmul(
                    out=spread[:],
                    lhsT=pick[:, gate : gate + 1].to_broadcast([P, P]),
                    rhs=bias_rows[:, cols],
                    start=True,
                    stop=True,
                )
                nc.scalar.copy(out=bias_gap[:, gate, cols], in_=spread[:])

        q_codes = keep.tile([P, PASSES, BATCH], U32, align_bytes=64)
        q_scales = keep.tile([P, PASSES, BATCH], U8, align_bytes=64)
        words_in = rows_in[:].bitcast(F32)
        words_per_pass = K_PASS // 2
        q_grouped_of = {}

        def quantise_q(g):
            nc.vector.quantize_mx(
                out=q_codes[:, g, :].bitcast(FP8X4), scales=q_scales[:, g, :], in_=q_grouped_of[g][:]
            )

        def turn_q(g):
            s = 1 + (g * K_PASS) // UNITS
            first_word = ((g * K_PASS) % UNITS) // 2
            turned = bank([P, BATCH_TILES, 2, P], F32, 4 + g % 4)
            for m in range(BATCH_TILES):
                pass_words = words_in[:, s, m, first_word : first_word + words_per_pass].rearrange(
                    "b (p u) -> b u p", u=2
                )
                for u in range(2):
                    nc.tensor.transpose(turned[:, m, u, :], pass_words[:, u, :], ident_f32[:])
            q_grouped = q_stage.tile([P, BATCH * PACK], BF16, align_bytes=64)
            side_by_side = q_grouped[:].bitcast(F32).rearrange("p (m b u) -> p m b u", m=BATCH_TILES, u=2)
            nc.scalar.copy(out=side_by_side, in_=turned[:].rearrange("p m u b -> p m b u"))
            q_grouped_of[g] = q_grouped

        grouped_of = {}
        codes_of = {}
        sums = {}

        def pieces_of(c):
            b = units[c][0]
            members = [i for i in range(len(units)) if units[i][0] == b]
            low, high = BLOCKS[b][3]
            share = low + (high - low) * members.index(c) / (len(members) - 1)
            shares = []
            for start, width, part in raw_of[c]:
                mine = int(width * share) // 8 * 8
                shares.append((start, part, 0, mine, width))
            return shares

        def regroup(copy, run, c, start, part, lo, hi):
            copy(
                out=grouped_of[c][:, start + lo : start + hi, :].rearrange("p (c i) t -> p c t i", i=run),
                in_=part[:, :, lo:hi].rearrange("p t (c i) -> p c t i", i=run),
            )

        marks = keep.tile([P, MARKS, MARK_PITCH], F32)
        gpsimd_cols = {}

        def grouped_tile(c):
            if c not in grouped_of:
                grouped_of[c] = grouped_pool.tile([P, UNITS, PACK], BF16, align_bytes=64, name="grouped")
            return grouped_of[c]

        def regroup_gpsimd(i, jobs):
            mark = marks[:, i, 0:1]
            nc.vector.memset(mark, 1.0)
            for c, cols in jobs:
                gpsimd_cols[c] = cols
                start, width, part = raw_of[c][-1]
                nc.gpsimd.tensor_scalar(
                    out=grouped_tile(c)[:, UNITS - cols : UNITS, :],
                    in0=part[:, :, width - cols : width].rearrange("p t w -> p w t"),
                    scalar1=mark,
                    scalar2=0.0,
                    op0=ALU.mult,
                    op1=ALU.add,
                )

        def regroup_scalar(c):
            grouped_tile(c)
            for start, part, lo, mid, hi in pieces_of(c):
                if start + hi == UNITS:
                    hi -= gpsimd_cols.get(c, 0)
                regroup(nc.scalar.copy, SCALAR_RUN, c, start, part, mid, hi)

        def regroup_vector(c):
            for start, part, lo, mid, hi in pieces_of(c):
                regroup(nc.vector.tensor_copy, VECTOR_RUN, c, start, part, lo, mid)

        def quantise(c):
            w_codes = code_pool.tile([P, UNITS], U32, align_bytes=64, name="w_codes")
            w_scales = code_pool.tile([P, UNITS], U8, align_bytes=64, name="w_scales")
            pieces = LAST_PIECES if c == len(units) - 1 else 1
            piece = UNITS // pieces
            for i in range(pieces):
                cols = slice(i * piece, (i + 1) * piece)
                nc.vector.quantize_mx(
                    out=w_codes[:, cols].bitcast(FP8X4),
                    scales=w_scales[:, cols],
                    in_=grouped_of[c][:, cols, :].rearrange("p w t -> p (w t)"),
                )
            codes_of[c] = (w_codes, w_scales)

        def multiply(c):
            b, parts = units[c]
            gate = BLOCKS[b][0]
            w_codes, w_scales = codes_of[c]
            start = 0
            for g, first, width in parts:
                for m in range(BATCH_TILES):
                    rows = slice(m * P, (m + 1) * P)
                    for i in range(width // HALF):
                        h = first // HALF + i
                        cols = slice(start + i * HALF, start + (i + 1) * HALF)
                        if g == 0:
                            index = FIRST_BANK[b] + m * (width // HALF) + i
                            sums[(gate, h, m)] = bank([P, HALF], F32, index)
                        nc.tensor.matmul_mx(
                            out=sums[(gate, h, m)][:],
                            lhsT=q_codes[:, g, rows].bitcast(FP8X4),
                            lhsT_scale=q_scales[:, g, rows],
                            rhs=w_codes[:, cols].bitcast(FP8X4),
                            rhs_scale=w_scales[:, cols],
                            start=(g == 0),
                            stop=(g == PASSES - 1),
                        )
                start += width

        tensor_tensor = nc.vector.tensor_tensor
        shape = [P, BATCH_TILES, HALF]
        logits = {}
        peak = {}
        total = {}
        mean = {}
        gap = {}
        lean = {}

        for h in range(HALVES):
            logits[h] = keep.tile([P, LAST, BATCH_TILES, HALF], F32, name="logits%d" % h)
            peak[h] = keep.tile(shape, F32, name="peak%d" % h)

        def add_bias(gate, h):
            cols = slice(h * HALF, (h + 1) * HALF)
            for m in range(BATCH_TILES):
                tensor_tensor(
                    out=logits[h][:, gate, m, :],
                    in0=sums[(gate, h, m)][:],
                    in1=bias_gap[:, gate, cols],
                    op=ALU.add,
                )

        def peak_two(h):
            tensor_tensor(out=peak[h][:], in0=logits[h][:, 0, :, :], in1=logits[h][:, 1, :, :], op=ALU.max)

        def peak_three(h):
            tensor_tensor(out=peak[h][:], in0=peak[h][:], in1=logits[h][:, 2, :, :], op=ALU.max)

        def subtract_peak(h):
            for gate in range(LAST):
                tensor_tensor(
                    out=logits[h][:, gate, :, :], in0=logits[h][:, gate, :, :], in1=peak[h][:], op=ALU.subtract
                )

        def exponentials(h):
            for gate in range(LAST):
                nc.scalar.activation(out=logits[h][:, gate, :, :], in_=logits[h][:, gate, :, :], func=ACT.Exp)

        def weigh(h):
            cols = slice(h * HALF, (h + 1) * HALF)
            weighted[h] = scratch.tile([P, LAST, BATCH_TILES, HALF], F32, name="weighted%d" % h)
            for gate in range(LAST):
                tensor_tensor(
                    out=weighted[h][:, gate, :, :],
                    in0=logits[h][:, gate, :, :],
                    in1=rows_in[:, gate, :, cols],
                    op=ALU.mult,
                )

        weighted = {}

        turned_shape = [P, HALF // P, P]

        def add_up(first, terms):
            added = {}
            for m in range(BATCH_TILES):
                added[m] = bank(turned_shape, F32, first + m)
                for j in range(HALF // P):
                    for gate in range(LAST):
                        nc.tensor.matmul(
                            out=added[m][:, j, :],
                            lhsT=terms[:, gate, m, j * P : (j + 1) * P],
                            rhs=ident_f32[:],
                            start=(gate == 0),
                            stop=(gate == LAST - 1),
                            is_transpose=True,
                        )
            return added

        def turn_back(first, turned, cols=None):
            back = {}
            for m in range(BATCH_TILES):
                back[m] = bank([P, HALF], F32, first + m)
                if cols is not None:
                    nc.tensor.matmul(
                        out=back[m][:], lhsT=ident_bf16[:], rhs=rows_in[:, LAST, m, cols], start=True, stop=False
                    )
            for m in range(BATCH_TILES):
                for j in range(HALF // P):
                    block = slice(j * P, (j + 1) * P)
                    nc.tensor.matmul(
                        out=back[m][:, block],
                        lhsT=turned[:, m, block],
                        rhs=ident_f32[:],
                        start=(cols is None),
                        stop=(cols is None or block.stop == HALF),
                        is_transpose=True,
                    )
            return back

        totals = {}
        blends = {}
        log_back = {}

        def add_weights(h):
            totals[h] = add_up(BATCH_TILES * h, logits[h])

        def add_products(h):
            blends[h] = add_up(6 - 6 * h, weighted[h])
            mean[h] = weighted[h][:, 0, :, :]

        def logarithm(h):
            gap[h] = logits[h][:, 1, :, :]
            for m in range(BATCH_TILES):
                nc.scalar.activation(
                    out=gap[h][:, m, :], in_=totals[h][m][:].rearrange("p j b -> p (j b)"), func=ACT.Ln
                )
            log_back[h] = turn_back(BATCH_TILES * h, gap[h])

        def one_over_total(h):
            total[h] = logits[h][:, 0, :, :]
            nc.scalar.activation(out=total[h], in_=gap[h], func=ACT.Exp, scale=-1.0)

        def minus_lse(h):
            gap[h] = logits[h][:, 2, :, :]
            for m in range(BATCH_TILES):
                nc.vector.scalar_tensor_tensor(
                    out=gap[h][:, m, :], in0=peak[h][:, m, :], scalar=-1.0, in1=log_back[h][m][:],
                    op0=ALU.mult, op1=ALU.subtract,
                )

        def divide(h):
            for m in range(BATCH_TILES):
                nc.vector.scalar_tensor_tensor(
                    out=mean[h][:, m, :], in0=blends[h][m][:].rearrange("p j b -> p (j b)"), scalar=-1.0,
                    in1=total[h][:, m, :], op0=ALU.mult, op1=ALU.mult,
                )
            lean[h] = turn_back(6 - 6 * h, mean[h], slice(h * HALF, (h + 1) * HALF))

        def last_gate(h):
            for m in range(BATCH_TILES):
                tensor_tensor(
                    out=gap[h][:, m, :], in0=sums[(LAST, h, m)][:], in1=gap[h][:, m, :], op=ALU.add
                )
                nc.scalar.activation(out=gap[h][:, m, :], in_=gap[h][:, m, :], func=ACT.Tanh, scale=0.5)

        def join_and_store(h):
            cols = slice(h * HALF, (h + 1) * HALF)
            for m in range(BATCH_TILES):
                nc.vector.scalar_tensor_tensor(
                    out=gap[h][:, m, :], in0=gap[h][:, m, :], scalar=-1.0, in1=lean[h][m][:],
                    op0=ALU.add, op1=ALU.mult,
                )
            for m in range(BATCH_TILES):
                nc.vector.scalar_tensor_tensor(
                    out=mean[h][:, m, :], in0=gap[h][:, m, :], scalar=0.5, in1=rows_in[:, LAST, m, cols],
                    op0=ALU.mult, op1=ALU.add,
                )
                nc.sync.dma_start(out=out[m * P : (m + 1) * P, cols], in_=mean[h][:, m, :])

        plan = {}

        def at(turn, fn, *args):
            plan.setdefault(turn, []).append((fn, args))

        end = {}
        for c, (b, parts) in enumerate(units):
            end[b] = c + 3
        at(end[0] + Q_LAG - 1, regroup_gpsimd, 0, [(end[0] + Q_LAG, LONG_STRETCH)])
        at(end[1], regroup_gpsimd, 1, [(end[1] + 1, LONG_STRETCH)])
        for h in range(HALVES):
            at(end[0] + Q_LAG - 1, add_bias, 0, h)
            at(end[1], add_bias, 1, h)
            at(end[1] + 1 + h, peak_two, h)
        for h in range(HALVES):
            t = end[2 + h]
            at(t, regroup_gpsimd, 2 + h, [(t + 1, SHORT_STRETCH)])
            at(t, add_bias, 2, h)
            at(t, peak_three, h)
            at(t + h, subtract_peak, h)
            at(t + 1, exponentials, h)
            at(t + 1 + h, add_weights, h)
            at(t + 1, weigh, h)
        at(end[2] + 3, add_products, 0)
        t = end[3] + 2
        for fn in (logarithm, one_over_total):
            for h in range(HALVES):
                at(t, fn, h)
        at(t + 1, regroup_gpsimd, 4, [(t + 2, LSE_STRETCH), (t + 3, LSE_STRETCH)])
        for h in range(HALVES):
            at(t + 1, minus_lse, h)
        at(t + 1, add_products, 1)
        for h in range(HALVES):
            at(t + 1, divide, h)
        at(end[4] + 1, last_gate, 0)
        at(end[4] + 2, join_and_store, 0)
        at(end[5], last_gate, 1)
        at(end[5], join_and_store, 1)

        count = len(units)
        multiplied = 0
        for c in range(max(max(plan) + 1, count + 2)):
            ahead = c + PREFETCH
            if ahead < count:
                load_ahead(ahead)
            if c == 2 * PASSES:
                load_row_set(0)
            if Q_LAG <= c < PASSES + Q_LAG:
                turn_q(c - Q_LAG)
            if 1 <= c <= LAST:
                spread_bias(c - 1)
            if c < count:
                regroup_scalar(c)
                regroup_vector(c)
            if 1 <= c <= count:
                quantise(c - 1)
            if Q_LAG <= c < PASSES + Q_LAG:
                quantise_q(c - Q_LAG)
            while multiplied < min(count, c - 1) and (multiplied >= PASSES or multiplied < c - Q_LAG):
                multiply(multiplied)
                multiplied += 1
            for fn, args in plan.get(c, []):
                fn(*args)
